import numpy as np
import ml_dtypes


def mxq(x, axis, fmt="e4m3"):
    dtype, down = {"e4m3": (ml_dtypes.float8_e4m3fn, 7), "e5m2": (ml_dtypes.float8_e5m2, 14)}[fmt]
    v = np.moveaxis(np.asarray(x, np.float32).astype(ml_dtypes.bfloat16).astype(np.float64), axis, -1)
    blocks = v.reshape(v.shape[:-1] + (-1, 32))
    amax = np.abs(blocks).max(-1, keepdims=True)
    byte = np.maximum(np.where(amax > 0, np.frexp(amax)[1] - 1 + 127, 0) - down, 1)
    scale = np.exp2(byte - 127.0)
    codes = (blocks / scale).astype(np.float32).astype(dtype).astype(np.float64)
    return np.moveaxis((codes * scale).reshape(v.shape), -1, axis)


WIDE = False


def mx_kscale(k):
    if not WIDE:
        return np.ones(k)
    levels = np.array([10, -10, 5, -5, 0])
    a = np.random.permutation(np.resize(levels, k // 512 * 4)).reshape(k // 512, 4)
    idx = np.arange(k)
    return np.exp2(a[idx // 512, idx % 128 // 32])


BF16 = ml_dtypes.bfloat16


def bf(x):
    return np.asarray(x, np.float32).astype(BF16)


def f64(x):
    return np.asarray(x).astype(np.float64)


B, DD, DK, CI, CO, L, NLC, PAD, KL = 1, 2, 2, 512, 32, 128, 4, 4, 9


def seg_lengths():
    cover = (L + PAD + PAD) // NLC - PAD - PAD
    lens = [cover] * NLC
    lens[-1] = L - cover * (NLC - 1)
    return lens


def setup_inputs():
    s = mx_kscale(CI)
    x = np.random.standard_normal((B, DD, DK, CI, L)) * s[:, None]
    weight = np.random.standard_normal((DD, DK, CO, CI, NLC, KL)) / np.sqrt(CI * KL) / s[:, None, None]
    bias = np.random.standard_normal((DD, DK, CO, NLC)) * 0.5
    return {"x": bf(x), "weight": bf(weight[..., None, :]), "conv_bias_param": bf(bias[..., None])}


def reference(x, weight, conv_bias_param):
    xq = mxq(f64(x), 3, "e4m3")
    wq = mxq(f64(weight), 3, "e4m3")
    bias = f64(conv_bias_param)
    outs, start = [], 0
    for i, ln in enumerate(seg_lengths()):
        acc = np.zeros((B, DD, DK, CO, ln))
        for f in range(KL):
            lo = max(start, PAD - f)
            hi = min(start + ln, L + PAD - f)
            xs = xq[..., lo + f - PAD:hi + f - PAD].swapaxes(-1, -2)
            wf = wq[:, :, :, :, i, 0, f].swapaxes(-1, -2)
            acc[..., lo - start:hi - start] += (xs @ wf).swapaxes(-1, -2)
        outs.append(acc + bias[None, :, :, :, i, :])
        start += ln
    return np.concatenate(outs, axis=-1)

@@ -1,0 +1,146 @@
+import concourse.mybir as mybir
+from concourse.masks import make_identity
+
+BF16 = mybir.dt.bfloat16
+F32 = mybir.dt.float32
+U32 = mybir.dt.uint32
+U8 = mybir.dt.uint8
+FP8X4 = mybir.dt.float8_e4m3fn_x4
+
+P = 128
+PACK = 4
+GROUPS = 4
+CI = 512
+CO = 32
+L = 128
+SEGMENTS = 4
+TAPS = 9
+PAD = 4
+SEG_START = (0, 26, 52, 78, 128)
+
+ROWS = CO * PACK
+HALVES = 2
+HALF_ROWS = ROWS // HALVES
+TAP_RUN = 3
+STEP = 16
+PHASES = L // STEP
+
+FLOPS = 2 * GROUPS * CO * L * CI * TAPS
+
+
+def tile_partiallyunsharedconv1d_pa_s_kernel(tc, x, weight, conv_bias_param, out):
+    nc = tc.nc
+
+    x_view = x.rearrange("b d k (p j) l -> p (b d k) (j l)", j=PACK)
+    w_view = weight.rearrange("d k o (p j) s u f -> (d k) p o (j s u f)", j=PACK)
+    bias_view = conv_bias_param.rearrange("d k o s u -> (d k) (o s u)")
+    out_view = out.rearrange("b d k o l -> (b d k) o l")
+
+    with tc.tile_pool(name="keep", bufs=1) as keep, tc.psum_pool(name="psum", bufs=1) as psum:
+        x_raw = keep.tile([P, GROUPS, PACK, L], BF16)
+        x_grouped = keep.tile([P, GROUPS, 2 * L, PACK], BF16, align_bytes=64)
+        x_codes = keep.tile([P, GROUPS, 2 * L], U32, align_bytes=64)
+        x_scales = keep.tile([P, GROUPS, 2 * L], U8, align_bytes=64)
+
+        w_raw = keep.tile([P, GROUPS, ROWS, SEGMENTS, TAPS], BF16)
+        w_grouped = keep.tile([P, GROUPS, TAPS, SEGMENTS, ROWS], BF16, align_bytes=64)
+        w_codes = keep.tile([P, GROUPS, TAPS, SEGMENTS * CO], U32, align_bytes=64)
+        w_scales = keep.tile([P, GROUPS, TAPS, SEGMENTS * CO], U8, align_bytes=64)
+
+        bias_rows = keep.tile([P, CO, SEGMENTS], BF16)
+        bias_sorted = keep.tile([P, SEGMENTS, CO], BF16)
+        bias_column = keep.tile([P, GROUPS], F32)
+        identity = keep.tile([P, P], BF16)
+        result = keep.tile([P, GROUPS, L], F32)
+
+        nc.sync.dma_start(out=x_raw[:].rearrange("p g j l -> p g (j l)"), in_=x_view)
+        nc.vector.memset(bias_rows[:], 0.0)
+        nc.scalar.dma_start(
+            out=bias_rows[0:GROUPS].rearrange("g o s -> g (o s)"), in_=bias_view
+        )
+        for g in range(GROUPS):
+            for h in range(HALVES):
+                rows = slice(h * HALF_ROWS, (h + 1) * HALF_ROWS)
+                channels = slice(h * CO // HALVES, (h + 1) * CO // HALVES)
+                nc.sync.dma_start(
+                    out=w_raw[:, g, rows].rearrange("p (o j) s f -> p o (j s f)", j=PACK),
+                    in_=w_view[g, :, channels, :],
+                )
+
+        make_identity(nc, identity[:])
+        nc.vector.tensor_copy(out=bias_sorted[:], in_=bias_rows[:].rearrange("p o s -> p s o"))
+        bias_t = psum.tile([P, P], BF16)
+        nc.tensor.transpose(
+            bias_t[:], bias_sorted[:].rearrange("p s o -> p (s o)"), identity[:]
+        )
+        nc.vector.tensor_copy(out=bias_column[:], in_=bias_t[:, 0:GROUPS])
+
+        nc.vector.memset(x_grouped[:, :, 0:L, :], 0.0)
+        nc.vector.tensor_copy(
+            out=x_grouped[:, :, L : 2 * L, :].rearrange("p g (r q) j -> p g r q j", q=STEP),
+            in_=x_raw[:].rearrange("p g j (q r) -> p g r q j", r=PHASES),
+        )
+        nc.vector.quantize_mx(
+            out=x_codes[:].rearrange("p g l -> p (g l)").bitcast(FP8X4),
+            scales=x_scales[:].rearrange("p g l -> p (g l)"),
+            in_=x_grouped[:].rearrange("p g l j -> p (g l j)"),
+        )
+
+        for g in range(GROUPS):
+            for h in range(HALVES):
+                rows = slice(h * HALF_ROWS, (h + 1) * HALF_ROWS)
+                for f0 in range(0, TAPS, TAP_RUN):
+                    taps = slice(f0, f0 + TAP_RUN)
+                    nc.vector.tensor_copy(
+                        out=w_grouped[:, g, taps, 0:2, rows].rearrange("p f s r -> p s r f"),
+                        in_=w_raw[:, g, rows, 0:2, taps].rearrange("p r s f -> p s r f"),
+                    )
+                    nc.scalar.copy(
+                        out=w_grouped[:, g, taps, 2:4, rows].rearrange("p f s r -> p s r f"),
+                        in_=w_raw[:, g, rows, 2:4, taps].rearrange("p r s f -> p s r f"),
+                    )
+
+            acc = psum.tile([P, 2 * L], F32, name="acc%d" % g)
+            for f in range(TAPS):
+                nc.vector.quantize_mx(
+                    out=w_codes[:, g, f, :].bitcast(FP8X4),
+                    scales=w_scales[:, g, f, :],
+                    in_=w_grouped[:, g, f].rearrange("p s r -> p (s r)"),
+                )
+                first = 0 if f == 0 else L
+                nc.tensor.matmul_mx(
+                    out=acc[:, first - f * STEP : 2 * L - f * STEP],
+                    lhsT=w_codes[:, g, f, :].bitcast(FP8X4),
+                    lhsT_scale=w_scales[:, g, f, :],
+                    rhs=x_codes[:, g, first : 2 * L].bitcast(FP8X4),
+                    rhs_scale=x_scales[:, g, first : 2 * L],
+                    start=(f == 0),
+                    stop=(f == TAPS - 1),
+                )
+
+            acc_rows = acc[:].rearrange("p (a q) -> p q a", q=STEP)
+            res = result[:, g, :].rearrange("p (q r) -> p q r", r=PHASES)
+            nc.vector.tensor_scalar_add(
+                out=res,
+                in0=acc_rows[:, :, PAD : PAD + PHASES],
+                scalar1=bias_column[:, g : g + 1],
+            )
+            nc.vector.tensor_tensor(
+                out=res[:, 1:STEP, 0:PAD],
+                in0=acc_rows[:, 0 : STEP - 1, PAD + PHASES : 2 * PHASES],
+                in1=res[:, 1:STEP, 0:PAD],
+                op=mybir.AluOpType.add,
+            )
+            nc.vector.tensor_tensor(
+                out=res[:, 0 : STEP - 1, PAD:PHASES],
+                in0=acc_rows[:, 1:STEP, 0:PAD],
+                in1=res[:, 0 : STEP - 1, PAD:PHASES],
+                op=mybir.AluOpType.add,
+            )
+
+            for s in range(SEGMENTS):
+                positions = slice(SEG_START[s], SEG_START[s + 1])
+                nc.sync.dma_start(
+                    out=out_view[g, :, positions],
+                    in_=result[s * CO : (s + 1) * CO, g, positions],
+                )

@@ -18,10 +18,8 @@ TAPS = 9
 PAD = 4
 SEG_START = (0, 26, 52, 78, 128)
 
-ROWS = CO * PACK
-HALVES = 2
-HALF_ROWS = ROWS // HALVES
-TAP_RUN = 3
+TAP_COLS = SEGMENTS * CO * PACK
+BANK_TAPS = 2
 STEP = 16
 PHASES = L // STEP
 
@@ -31,19 +29,21 @@ FLOPS = 2 * GROUPS * CO * L * CI * TAPS
 def tile_partiallyunsharedconv1d_pa_s_kernel(tc, x, weight, conv_bias_param, out):
     nc = tc.nc
 
-    x_view = x.rearrange("b d k (p j) l -> p (b d k) (j l)", j=PACK)
-    w_view = weight.rearrange("d k o (p j) s u f -> (d k) p o (j s u f)", j=PACK)
+    x_view = x.rearrange("b d k (j p) l -> p (b d k j) l", p=P)
+    w_view = weight.rearrange("d k o (j c) s u f -> (d k) (o j) (c s u f)", j=PACK)
     bias_view = conv_bias_param.rearrange("d k o s u -> (d k) (o s u)")
     out_view = out.rearrange("b d k o l -> (b d k) o l")
 
-    with tc.tile_pool(name="keep", bufs=1) as keep, tc.psum_pool(name="psum", bufs=1) as psum:
+    with tc.tile_pool(name="keep", bufs=1) as keep, tc.psum_pool(
+        name="turned", bufs=6
+    ) as turned, tc.psum_pool(name="sums", bufs=2) as sums:
         x_raw = keep.tile([P, GROUPS, PACK, L], BF16)
         x_grouped = keep.tile([P, GROUPS, 2 * L, PACK], BF16, align_bytes=64)
         x_codes = keep.tile([P, GROUPS, 2 * L], U32, align_bytes=64)
         x_scales = keep.tile([P, GROUPS, 2 * L], U8, align_bytes=64)
 
-        w_raw = keep.tile([P, GROUPS, ROWS, SEGMENTS, TAPS], BF16)
-        w_grouped = keep.tile([P, GROUPS, TAPS, SEGMENTS, ROWS], BF16, align_bytes=64)
+        w_raw = keep.tile([P, GROUPS, P, SEGMENTS * TAPS], BF16)
+        w_grouped = keep.tile([P, GROUPS, TAPS, TAP_COLS], BF16, align_bytes=64)
         w_codes = keep.tile([P, GROUPS, TAPS, SEGMENTS * CO], U32, align_bytes=64)
         w_scales = keep.tile([P, GROUPS, TAPS, SEGMENTS * CO], U8, align_bytes=64)
 
@@ -53,60 +53,43 @@ def tile_partiallyunsharedconv1d_pa_s_kernel(tc, x, weight, conv_bias_param, out
         identity = keep.tile([P, P], BF16)
         result = keep.tile([P, GROUPS, L], F32)
 
-        nc.sync.dma_start(out=x_raw[:].rearrange("p g j l -> p g (j l)"), in_=x_view)
+        def load_weights(g):
+            nc.sync.dma_start(out=w_raw[:, g].rearrange("p c n -> p (c n)"), in_=w_view[g])
+
+        load_weights(0)
+        nc.sync.dma_start(out=x_raw[:].rearrange("p g j l -> p (g j) l"), in_=x_view)
+        for g in range(1, GROUPS):
+            load_weights(g)
         nc.vector.memset(bias_rows[:], 0.0)
         nc.scalar.dma_start(
             out=bias_rows[0:GROUPS].rearrange("g o s -> g (o s)"), in_=bias_view
         )
-        for g in range(GROUPS):
-            for h in range(HALVES):
-                rows = slice(h * HALF_ROWS, (h + 1) * HALF_ROWS)
-                channels = slice(h * CO // HALVES, (h + 1) * CO // HALVES)
-                nc.sync.dma_start(
-                    out=w_raw[:, g, rows].rearrange("p (o j) s f -> p o (j s f)", j=PACK),
-                    in_=w_view[g, :, channels, :],
+
+        def turn_weights(g):
+            for f0 in range(0, TAPS, BANK_TAPS):
+                taps = min(BANK_TAPS, TAPS - f0)
+                bank = turned.tile([P, BANK_TAPS * TAP_COLS], BF16, name="bank")
+                for t in range(taps):
+                    for s in range(SEGMENTS):
+                        first = (t * SEGMENTS + s) * P
+                        nc.tensor.transpose(
+                            bank[:, first : first + P],
+                            w_raw[:, g, :, s * TAPS + f0 + t],
+                            identity[:],
+                        )
+                nc.scalar.copy(
+                    out=w_grouped[:, g, f0 : f0 + taps].rearrange("p f n -> p (f n)"),
+                    in_=bank[:, 0 : taps * TAP_COLS],
                 )
-
-        make_identity(nc, identity[:])
-        nc.vector.tensor_copy(out=bias_sorted[:], in_=bias_rows[:].rearrange("p o s -> p s o"))
-        bias_t = psum.tile([P, P], BF16)
-        nc.tensor.transpose(
-            bias_t[:], bias_sorted[:].rearrange("p s o -> p (s o)"), identity[:]
-        )
-        nc.vector.tensor_copy(out=bias_column[:], in_=bias_t[:, 0:GROUPS])
-
-        nc.vector.memset(x_grouped[:, :, 0:L, :], 0.0)
-        nc.vector.tensor_copy(
-            out=x_grouped[:, :, L : 2 * L, :].rearrange("p g (r q) j -> p g r q j", q=STEP),
-            in_=x_raw[:].rearrange("p g j (q r) -> p g r q j", r=PHASES),
-        )
-        nc.vector.quantize_mx(
-            out=x_codes[:].rearrange("p g l -> p (g l)").bitcast(FP8X4),
-            scales=x_scales[:].rearrange("p g l -> p (g l)"),
-            in_=x_grouped[:].rearrange("p g l j -> p (g l j)"),
-        )
-
-        for g in range(GROUPS):
-            for h in range(HALVES):
-                rows = slice(h * HALF_ROWS, (h + 1) * HALF_ROWS)
-                for f0 in range(0, TAPS, TAP_RUN):
-                    taps = slice(f0, f0 + TAP_RUN)
-                    nc.vector.tensor_copy(
-                        out=w_grouped[:, g, taps, 0:2, rows].rearrange("p f s r -> p s r f"),
-                        in_=w_raw[:, g, rows, 0:2, taps].rearrange("p r s f -> p s r f"),
-                    )
-                    nc.scalar.copy(
-                        out=w_grouped[:, g, taps, 2:4, rows].rearrange("p f s r -> p s r f"),
-                        in_=w_raw[:, g, rows, 2:4, taps].rearrange("p r s f -> p s r f"),
-                    )
-
-            acc = psum.tile([P, 2 * L], F32, name="acc%d" % g)
-            for f in range(TAPS):
                 nc.vector.quantize_mx(
-                    out=w_codes[:, g, f, :].bitcast(FP8X4),
-                    scales=w_scales[:, g, f, :],
-                    in_=w_grouped[:, g, f].rearrange("p s r -> p (s r)"),
+                    out=w_codes[:, g, f0 : f0 + taps].rearrange("p f n -> p (f n)").bitcast(FP8X4),
+                    scales=w_scales[:, g, f0 : f0 + taps].rearrange("p f n -> p (f n)"),
+                    in_=w_grouped[:, g, f0 : f0 + taps].rearrange("p f n -> p (f n)"),
                 )
+
+        def convolve(g):
+            acc = sums.tile([P, 2 * L], F32, name="acc")
+            for f in range(TAPS):
                 first = 0 if f == 0 else L
                 nc.tensor.matmul_mx(
                     out=acc[:, first - f * STEP : 2 * L - f * STEP],
@@ -144,3 +127,30 @@ def tile_partiallyunsharedconv1d_pa_s_kernel(tc, x, weight, conv_bias_param, out
                     out=out_view[g, :, positions],
                     in_=result[s * CO : (s + 1) * CO, g, positions],
                 )
+
+        with tc.manual_schedule(engines={mybir.EngineType.PE}):
+            make_identity(nc, identity[:])
+            nc.scalar.copy(out=bias_sorted[:], in_=bias_rows[:].rearrange("p o s -> p s o"))
+            bias_t = turned.tile([P, BANK_TAPS * TAP_COLS], BF16, name="bank")
+            nc.tensor.transpose(
+                bias_t[:, 0:P], bias_sorted[:].rearrange("p s o -> p (s o)"), identity[:]
+            )
+            nc.vector.tensor_copy(out=bias_column[:], in_=bias_t[:, 0:GROUPS])
+
+            turn_weights(0)
+
+            nc.vector.memset(x_grouped[:, :, 0:L, :], 0.0)
+            nc.vector.tensor_copy(
+                out=x_grouped[:, :, L : 2 * L, :].rearrange("p g (r q) j -> p g r q j", q=STEP),
+                in_=x_raw[:].rearrange("p g j (q r) -> p g r q j", r=PHASES),
+            )
+            nc.vector.quantize_mx(
+                out=x_codes[:].rearrange("p g l -> p (g l)").bitcast(FP8X4),
+                scales=x_scales[:].rearrange("p g l -> p (g l)"),
+                in_=x_grouped[:].rearrange("p g l j -> p (g l j)"),
+            )
+
+            for g in range(1, GROUPS):
+                turn_weights(g)
+                convolve(g - 1)
+            convolve(GROUPS - 1)

@@ -18,8 +18,12 @@ TAPS = 9
 PAD = 4
 SEG_START = (0, 26, 52, 78, 128)
 
-TAP_COLS = SEGMENTS * CO * PACK
-BANK_TAPS = 2
+ROWS = CO * PACK
+PAIRS = SEGMENTS * TAPS // 2
+BANK_WORDS = 4
+WORD_RUNS = ((0, 0, 0), (5, 1, 1), (9, 2, 0), (14, 3, 1))
+STRADDLING = (4, 13)
+VECTOR_RUN = 1
 STEP = 16
 PHASES = L // STEP
 
@@ -42,49 +46,54 @@ def tile_partiallyunsharedconv1d_pa_s_kernel(tc, x, weight, conv_bias_param, out
         x_codes = keep.tile([P, GROUPS, 2 * L], U32, align_bytes=64)
         x_scales = keep.tile([P, GROUPS, 2 * L], U8, align_bytes=64)
 
-        w_raw = keep.tile([P, GROUPS, P, SEGMENTS * TAPS], BF16)
-        w_grouped = keep.tile([P, GROUPS, TAPS, TAP_COLS], BF16, align_bytes=64)
+        w_raw = keep.tile([P, GROUPS, P * SEGMENTS * TAPS], BF16)
+        w_grouped = keep.tile([P, GROUPS, TAPS, SEGMENTS, ROWS], BF16, align_bytes=64)
         w_codes = keep.tile([P, GROUPS, TAPS, SEGMENTS * CO], U32, align_bytes=64)
         w_scales = keep.tile([P, GROUPS, TAPS, SEGMENTS * CO], U8, align_bytes=64)
 
-        bias_rows = keep.tile([P, CO, SEGMENTS], BF16)
-        bias_sorted = keep.tile([P, SEGMENTS, CO], BF16)
+        bias_rows = keep.tile([GROUPS, CO, SEGMENTS], BF16)
+        bias_sorted = keep.tile([P, SEGMENTS, CO], F32)
         bias_column = keep.tile([P, GROUPS], F32)
-        identity = keep.tile([P, P], BF16)
+        identity = keep.tile([P, P], F32)
         result = keep.tile([P, GROUPS, L], F32)
 
-        def load_weights(g):
-            nc.sync.dma_start(out=w_raw[:, g].rearrange("p c n -> p (c n)"), in_=w_view[g])
-
-        load_weights(0)
+        nc.sync.dma_start(out=bias_rows[:].rearrange("g o s -> g (o s)"), in_=bias_view)
+        nc.sync.dma_start(out=w_raw[:, 0], in_=w_view[0])
         nc.sync.dma_start(out=x_raw[:].rearrange("p g j l -> p (g j) l"), in_=x_view)
         for g in range(1, GROUPS):
-            load_weights(g)
-        nc.vector.memset(bias_rows[:], 0.0)
-        nc.scalar.dma_start(
-            out=bias_rows[0:GROUPS].rearrange("g o s -> g (o s)"), in_=bias_view
-        )
+            nc.sync.dma_start(out=w_raw[:, g], in_=w_view[g])
 
         def turn_weights(g):
-            for f0 in range(0, TAPS, BANK_TAPS):
-                taps = min(BANK_TAPS, TAPS - f0)
-                bank = turned.tile([P, BANK_TAPS * TAP_COLS], BF16, name="bank")
-                for t in range(taps):
-                    for s in range(SEGMENTS):
-                        first = (t * SEGMENTS + s) * P
-                        nc.tensor.transpose(
-                            bank[:, first : first + P],
-                            w_raw[:, g, :, s * TAPS + f0 + t],
-                            identity[:],
-                        )
-                nc.scalar.copy(
-                    out=w_grouped[:, g, f0 : f0 + taps].rearrange("p f n -> p (f n)"),
-                    in_=bank[:, 0 : taps * TAP_COLS],
+            words = w_raw[:, g].bitcast(F32).rearrange("p (c w) -> p c w", w=PAIRS)
+
+            def turn(word_list):
+                bank = turned.tile([P, BANK_WORDS * P], F32, name="bank")
+                for slot, w in enumerate(word_list):
+                    nc.tensor.transpose(
+                        bank[:, slot * P : (slot + 1) * P], words[:, :, w], identity[:]
+                    )
+                return bank[:].bitcast(BF16).rearrange(
+                    "p (w n e) -> p w e n", w=BANK_WORDS, e=2
                 )
+
+            for run, (w0, s, f0) in enumerate(WORD_RUNS):
+                halves = turn(range(w0, w0 + BANK_WORDS))
+                target = w_grouped[:, g, f0 : f0 + 2 * BANK_WORDS, s, :].rearrange(
+                    "p (w e) n -> p w e n", e=2
+                )
+                if run == VECTOR_RUN:
+                    nc.vector.tensor_copy(out=target, in_=halves)
+                else:
+                    nc.scalar.copy(out=target, in_=halves)
+            halves = turn(STRADDLING)
+            nc.scalar.copy(out=w_grouped[:, g, TAPS - 1, 0:SEGMENTS:2, :], in_=halves[:, 0:2, 0, :])
+            nc.scalar.copy(out=w_grouped[:, g, 0, 1:SEGMENTS:2, :], in_=halves[:, 0:2, 1, :])
+
+            for f in range(TAPS):
                 nc.vector.quantize_mx(
-                    out=w_codes[:, g, f0 : f0 + taps].rearrange("p f n -> p (f n)").bitcast(FP8X4),
-                    scales=w_scales[:, g, f0 : f0 + taps].rearrange("p f n -> p (f n)"),
-                    in_=w_grouped[:, g, f0 : f0 + taps].rearrange("p f n -> p (f n)"),
+                    out=w_codes[:, g, f, :].bitcast(FP8X4),
+                    scales=w_scales[:, g, f, :],
+                    in_=w_grouped[:, g, f].rearrange("p s n -> p (s n)"),
                 )
 
         def convolve(g):
@@ -130,8 +139,11 @@ def tile_partiallyunsharedconv1d_pa_s_kernel(tc, x, weight, conv_bias_param, out
 
         with tc.manual_schedule(engines={mybir.EngineType.PE}):
             make_identity(nc, identity[:])
-            nc.scalar.copy(out=bias_sorted[:], in_=bias_rows[:].rearrange("p o s -> p s o"))
-            bias_t = turned.tile([P, BANK_TAPS * TAP_COLS], BF16, name="bank")
+            nc.vector.memset(bias_sorted[:], 0.0)
+            nc.scalar.copy(
+                out=bias_sorted[0:GROUPS], in_=bias_rows[:].rearrange("g o s -> g s o")
+            )
+            bias_t = turned.tile([P, BANK_WORDS * P], F32, name="bank")
             nc.tensor.transpose(
                 bias_t[:, 0:P], bias_sorted[:].rearrange("p s o -> p (s o)"), identity[:]
             )

@@ -5,6 +5,7 @@ BF16 = mybir.dt.bfloat16
 F32 = mybir.dt.float32
 U32 = mybir.dt.uint32
 U8 = mybir.dt.uint8
+I32 = mybir.dt.int32
 FP8X4 = mybir.dt.float8_e4m3fn_x4
 
 P = 128
@@ -23,9 +24,18 @@ PAIRS = SEGMENTS * TAPS // 2
 BANK_WORDS = 4
 WORD_RUNS = ((0, 0, 0), (5, 1, 1), (9, 2, 0), (14, 3, 1))
 STRADDLING = (4, 13)
-VECTOR_RUN = 1
+
+TURNED = (0, 1)
+REGROUPED = (2, 3)
+HALVES = 2
+HALF_ROWS = ROWS // HALVES
+REGROUPED_RUNS = ((0, 4), (4, 4), (8, 1))
+TURNED_RUNS = ((0, 8), (8, 1))
+VECTOR_SEGMENTS = {2: 4, 3: 2}
 STEP = 16
 PHASES = L // STEP
+TABLE = (PHASES + TAPS - 1) * STEP
+PLANES = 64 // STEP
 
 FLOPS = 2 * GROUPS * CO * L * CI * TAPS
 
@@ -33,20 +43,22 @@ FLOPS = 2 * GROUPS * CO * L * CI * TAPS
 def tile_partiallyunsharedconv1d_pa_s_kernel(tc, x, weight, conv_bias_param, out):
     nc = tc.nc
 
-    x_view = x.rearrange("b d k (j p) l -> p (b d k j) l", p=P)
-    w_view = weight.rearrange("d k o (j c) s u f -> (d k) (o j) (c s u f)", j=PACK)
+    x_quarters = x.rearrange("b d k (j p) l -> p (b d k) j l", p=P)
+    x_fours = x.rearrange("b d k (p j) l -> p (b d k) (j l)", j=PACK)
+    w_quarters = weight.rearrange("d k o (j c) s u f -> (d k) (o j) (c s u f)", j=PACK)
+    w_fours = weight.rearrange("d k o (p j) s u f -> (d k) p o (j s u f)", j=PACK)
     bias_view = conv_bias_param.rearrange("d k o s u -> (d k) (o s u)")
     out_view = out.rearrange("b d k o l -> (b d k) o l")
 
     with tc.tile_pool(name="keep", bufs=1) as keep, tc.psum_pool(
-        name="turned", bufs=6
-    ) as turned, tc.psum_pool(name="sums", bufs=2) as sums:
+        name="turned", bufs=4
+    ) as turned, tc.psum_pool(name="sums", bufs=GROUPS) as sums:
         x_raw = keep.tile([P, GROUPS, PACK, L], BF16)
-        x_grouped = keep.tile([P, GROUPS, 2 * L, PACK], BF16, align_bytes=64)
-        x_codes = keep.tile([P, GROUPS, 2 * L], U32, align_bytes=64)
-        x_scales = keep.tile([P, GROUPS, 2 * L], U8, align_bytes=64)
+        x_grouped = keep.tile([P, GROUPS, TABLE, PACK], BF16, align_bytes=64)
+        x_codes = keep.tile([P, GROUPS, TABLE], U32, align_bytes=64)
+        x_scales = keep.tile([P, PLANES, GROUPS, TABLE], U8, align_bytes=64)
 
-        w_raw = keep.tile([P, GROUPS, P * SEGMENTS * TAPS], BF16)
+        w_raw = keep.tile([P, GROUPS, ROWS * SEGMENTS * TAPS], BF16)
         w_grouped = keep.tile([P, GROUPS, TAPS, SEGMENTS, ROWS], BF16, align_bytes=64)
         w_codes = keep.tile([P, GROUPS, TAPS, SEGMENTS * CO], U32, align_bytes=64)
         w_scales = keep.tile([P, GROUPS, TAPS, SEGMENTS * CO], U8, align_bytes=64)
@@ -58,10 +70,32 @@ def tile_partiallyunsharedconv1d_pa_s_kernel(tc, x, weight, conv_bias_param, out
         result = keep.tile([P, GROUPS, L], F32)
 
         nc.sync.dma_start(out=bias_rows[:].rearrange("g o s -> g (o s)"), in_=bias_view)
-        nc.sync.dma_start(out=w_raw[:, 0], in_=w_view[0])
-        nc.sync.dma_start(out=x_raw[:].rearrange("p g j l -> p (g j) l"), in_=x_view)
-        for g in range(1, GROUPS):
-            nc.sync.dma_start(out=w_raw[:, g], in_=w_view[g])
+
+        def load_turned(g):
+            nc.sync.dma_start(out=w_raw[:, g], in_=w_quarters[g])
+
+        def load_regrouped(g, h):
+            channels = slice(h * CO // HALVES, (h + 1) * CO // HALVES)
+            nc.sync.dma_start(
+                out=w_raw[:, g].rearrange("p (o n) -> p o n", o=CO)[:, channels, :],
+                in_=w_fours[g, :, channels, :],
+            )
+
+        groups = slice(TURNED[0], TURNED[-1] + 1)
+        nc.sync.dma_start(
+            out=x_raw[:, groups].rearrange("p g j l -> p (g j) l"),
+            in_=x_quarters[:, groups].rearrange("p g j l -> p (g j) l"),
+        )
+        groups = slice(REGROUPED[0], REGROUPED[-1] + 1)
+        nc.sync.dma_start(
+            out=x_raw[:, groups].rearrange("p g j l -> p g (j l)"), in_=x_fours[:, groups]
+        )
+        load_turned(TURNED[0])
+        load_regrouped(REGROUPED[0], 0)
+        load_turned(TURNED[1])
+        load_regrouped(REGROUPED[0], 1)
+        load_regrouped(REGROUPED[1], 0)
+        load_regrouped(REGROUPED[1], 1)
 
         def turn_weights(g):
             words = w_raw[:, g].bitcast(F32).rearrange("p (c w) -> p c w", w=PAIRS)
@@ -76,58 +110,61 @@ def tile_partiallyunsharedconv1d_pa_s_kernel(tc, x, weight, conv_bias_param, out
                     "p (w n e) -> p w e n", w=BANK_WORDS, e=2
                 )
 
-            for run, (w0, s, f0) in enumerate(WORD_RUNS):
+            for w0, s, f0 in WORD_RUNS:
                 halves = turn(range(w0, w0 + BANK_WORDS))
                 target = w_grouped[:, g, f0 : f0 + 2 * BANK_WORDS, s, :].rearrange(
                     "p (w e) n -> p w e n", e=2
                 )
-                if run == VECTOR_RUN:
-                    nc.vector.tensor_copy(out=target, in_=halves)
-                else:
-                    nc.scalar.copy(out=target, in_=halves)
+                nc.scalar.copy(out=target, in_=halves)
             halves = turn(STRADDLING)
             nc.scalar.copy(out=w_grouped[:, g, TAPS - 1, 0:SEGMENTS:2, :], in_=halves[:, 0:2, 0, :])
             nc.scalar.copy(out=w_grouped[:, g, 0, 1:SEGMENTS:2, :], in_=halves[:, 0:2, 1, :])
 
-            for f in range(TAPS):
+        def regroup_weights(g, h):
+            loaded = w_raw[:, g].rearrange("p (r s f) -> p r s f", s=SEGMENTS, f=TAPS)
+            split = VECTOR_SEGMENTS[g]
+            rows = slice(h * HALF_ROWS, (h + 1) * HALF_ROWS)
+            for f0, n in REGROUPED_RUNS:
+                taps = slice(f0, f0 + n)
+                nc.vector.tensor_copy(
+                    out=w_grouped[:, g, taps, 0:split, rows].rearrange("p f s r -> p s r f"),
+                    in_=loaded[:, rows, 0:split, taps].rearrange("p r s f -> p s r f"),
+                )
+                if split < SEGMENTS:
+                    nc.scalar.copy(
+                        out=w_grouped[:, g, taps, split:, rows].rearrange("p f s r -> p s r f"),
+                        in_=loaded[:, rows, split:, taps].rearrange("p r s f -> p s r f"),
+                    )
+
+        def quantise_weights(g, runs):
+            for f0, n in runs:
+                taps = slice(f0, f0 + n)
                 nc.vector.quantize_mx(
-                    out=w_codes[:, g, f, :].bitcast(FP8X4),
-                    scales=w_scales[:, g, f, :],
-                    in_=w_grouped[:, g, f].rearrange("p s n -> p (s n)"),
+                    out=w_codes[:, g, taps].rearrange("p f n -> p (f n)").bitcast(FP8X4),
+                    scales=w_scales[:, g, taps].rearrange("p f n -> p (f n)"),
+                    in_=w_grouped[:, g, taps].rearrange("p f s n -> p (f s n)"),
                 )
 
         def convolve(g):
-            acc = sums.tile([P, 2 * L], F32, name="acc")
+            acc = sums.tile([P, L], F32, name="acc")
             for f in range(TAPS):
-                first = 0 if f == 0 else L
+                plane = f % PLANES
                 nc.tensor.matmul_mx(
-                    out=acc[:, first - f * STEP : 2 * L - f * STEP],
+                    out=acc[:],
                     lhsT=w_codes[:, g, f, :].bitcast(FP8X4),
                     lhsT_scale=w_scales[:, g, f, :],
-                    rhs=x_codes[:, g, first : 2 * L].bitcast(FP8X4),
-                    rhs_scale=x_scales[:, g, first : 2 * L],
+                    rhs=x_codes[:, g, f * STEP : f * STEP + L].bitcast(FP8X4),
+                    rhs_scale=x_scales[:, plane, g, (f - plane) * STEP : (f - plane) * STEP + L],
                     start=(f == 0),
                     stop=(f == TAPS - 1),
                 )
+            return acc
 
-            acc_rows = acc[:].rearrange("p (a q) -> p q a", q=STEP)
-            res = result[:, g, :].rearrange("p (q r) -> p q r", r=PHASES)
+        def finish(g, acc):
             nc.vector.tensor_scalar_add(
-                out=res,
-                in0=acc_rows[:, :, PAD : PAD + PHASES],
+                out=result[:, g, :].rearrange("p (q r) -> p q r", r=PHASES),
+                in0=acc[:].rearrange("p (r q) -> p q r", q=STEP),
                 scalar1=bias_column[:, g : g + 1],
-            )
-            nc.vector.tensor_tensor(
-                out=res[:, 1:STEP, 0:PAD],
-                in0=acc_rows[:, 0 : STEP - 1, PAD + PHASES : 2 * PHASES],
-                in1=res[:, 1:STEP, 0:PAD],
-                op=mybir.AluOpType.add,
-            )
-            nc.vector.tensor_tensor(
-                out=res[:, 0 : STEP - 1, PAD:PHASES],
-                in0=acc_rows[:, 1:STEP, 0:PAD],
-                in1=res[:, 0 : STEP - 1, PAD:PHASES],
-                op=mybir.AluOpType.add,
             )
 
             for s in range(SEGMENTS):
@@ -137,7 +174,7 @@ def tile_partiallyunsharedconv1d_pa_s_kernel(tc, x, weight, conv_bias_param, out
                     in_=result[s * CO : (s + 1) * CO, g, positions],
                 )
 
-        with tc.manual_schedule(engines={mybir.EngineType.PE}):
+        with tc.manual_schedule():
             make_identity(nc, identity[:])
             nc.vector.memset(bias_sorted[:], 0.0)
             nc.scalar.copy(
@@ -149,20 +186,46 @@ def tile_partiallyunsharedconv1d_pa_s_kernel(tc, x, weight, conv_bias_param, out
             )
             nc.vector.tensor_copy(out=bias_column[:], in_=bias_t[:, 0:GROUPS])
 
-            turn_weights(0)
-
-            nc.vector.memset(x_grouped[:, :, 0:L, :], 0.0)
-            nc.vector.tensor_copy(
-                out=x_grouped[:, :, L : 2 * L, :].rearrange("p g (r q) j -> p g r q j", q=STEP),
-                in_=x_raw[:].rearrange("p g j (q r) -> p g r q j", r=PHASES),
+            table = x_grouped[:].rearrange("p g (a q) j -> p g a q j", q=STEP)
+            loaded = x_raw[:].rearrange("p g j (q r) -> p g r q j", r=PHASES)
+            nc.gpsimd.memset(table[:, :, 0:PAD], 0.0)
+            nc.gpsimd.memset(table[:, :, PAD + PHASES :], 0.0)
+            nc.vector.memset(x_scales[:, 0].rearrange("p g l -> p (g l)").bitcast(I32), 0)
+            nc.vector.tensor_copy(out=table[:, :, PAD : PAD + PHASES], in_=loaded)
+            nc.scalar.copy(
+                out=table[:, :, 0:PAD, 1:STEP], in_=loaded[:, :, PHASES - PAD :, 0 : STEP - 1]
+            )
+            nc.scalar.copy(
+                out=table[:, :, PAD + PHASES :, 0 : STEP - 1], in_=loaded[:, :, 0:PAD, 1:STEP]
             )
             nc.vector.quantize_mx(
                 out=x_codes[:].rearrange("p g l -> p (g l)").bitcast(FP8X4),
-                scales=x_scales[:].rearrange("p g l -> p (g l)"),
+                scales=x_scales[:, 0].rearrange("p g l -> p (g l)"),
                 in_=x_grouped[:].rearrange("p g l j -> p (g l j)"),
             )
+            for plane in range(1, PLANES):
+                nc.vector.tensor_copy(
+                    out=x_scales[:, plane, :, 0 : TABLE - plane * STEP].bitcast(I32),
+                    in_=x_scales[:, 0, :, plane * STEP : TABLE].bitcast(I32),
+                )
 
-            for g in range(1, GROUPS):
-                turn_weights(g)
-                convolve(g - 1)
-            convolve(GROUPS - 1)
+            t0, t1 = TURNED
+            r0, r1 = REGROUPED
+            turn_weights(t0)
+            regroup_weights(r0, 0)
+            quantise_weights(t0, TURNED_RUNS)
+            turn_weights(t1)
+            regroup_weights(r0, 1)
+            quantise_weights(r0, REGROUPED_RUNS)
+            acc_t0 = convolve(t0)
+            acc_r0 = convolve(r0)
+            regroup_weights(r1, 0)
+            finish(t0, acc_t0)
+            quantise_weights(t1, TURNED_RUNS)
+            acc_t1 = convolve(t1)
+            finish(r0, acc_r0)
+            regroup_weights(r1, 1)
+            finish(t1, acc_t1)
+            quantise_weights(r1, REGROUPED_RUNS)
+            acc_r1 = convolve(r1)
+            finish(r1, acc_r1)

@@ -54,7 +54,7 @@ def tile_partiallyunsharedconv1d_pa_s_kernel(tc, x, weight, conv_bias_param, out
         name="turned", bufs=4
     ) as turned, tc.psum_pool(name="sums", bufs=GROUPS) as sums:
         x_raw = keep.tile([P, GROUPS, PACK, L], BF16)
-        x_grouped = keep.tile([P, GROUPS, TABLE, PACK], BF16, align_bytes=64)
+        x_grouped = keep.tile([P, GROUPS, L, PACK], BF16, align_bytes=64)
         x_codes = keep.tile([P, GROUPS, TABLE], U32, align_bytes=64)
         x_scales = keep.tile([P, PLANES, GROUPS, TABLE], U8, align_bytes=64)
 
@@ -161,10 +161,11 @@ def tile_partiallyunsharedconv1d_pa_s_kernel(tc, x, weight, conv_bias_param, out
             return acc
 
         def finish(g, acc):
-            nc.vector.tensor_scalar_add(
+            nc.scalar.activation(
                 out=result[:, g, :].rearrange("p (q r) -> p q r", r=PHASES),
-                in0=acc[:].rearrange("p (r q) -> p q r", q=STEP),
-                scalar1=bias_column[:, g : g + 1],
+                in_=acc[:].rearrange("p (r q) -> p q r", q=STEP),
+                func=mybir.ActivationFunctionType.Identity,
+                bias=bias_column[:, g : g + 1],
             )
 
             for s in range(SEGMENTS):
@@ -186,23 +187,29 @@ def tile_partiallyunsharedconv1d_pa_s_kernel(tc, x, weight, conv_bias_param, out
             )
             nc.vector.tensor_copy(out=bias_column[:], in_=bias_t[:, 0:GROUPS])
 
-            table = x_grouped[:].rearrange("p g (a q) j -> p g a q j", q=STEP)
-            loaded = x_raw[:].rearrange("p g j (q r) -> p g r q j", r=PHASES)
-            nc.gpsimd.memset(table[:, :, 0:PAD], 0.0)
-            nc.gpsimd.memset(table[:, :, PAD + PHASES :], 0.0)
+            codes = x_codes[:].bitcast(I32).rearrange("p g (a q) -> p g a q", q=STEP)
+            scales = x_scales[:, 0].rearrange("p g (a q) -> p g a q", q=STEP)
+            nc.vector.memset(codes[:, :, 0:PAD], 0)
+            nc.vector.memset(codes[:, :, PAD + PHASES :], 0)
             nc.vector.memset(x_scales[:, 0].rearrange("p g l -> p (g l)").bitcast(I32), 0)
-            nc.vector.tensor_copy(out=table[:, :, PAD : PAD + PHASES], in_=loaded)
-            nc.scalar.copy(
-                out=table[:, :, 0:PAD, 1:STEP], in_=loaded[:, :, PHASES - PAD :, 0 : STEP - 1]
+            nc.vector.tensor_copy(
+                out=x_grouped[:].rearrange("p g (r q) j -> p g r q j", q=STEP),
+                in_=x_raw[:].rearrange("p g j (q r) -> p g r q j", r=PHASES),
             )
-            nc.scalar.copy(
-                out=table[:, :, PAD + PHASES :, 0 : STEP - 1], in_=loaded[:, :, 0:PAD, 1:STEP]
-            )
-            nc.vector.quantize_mx(
-                out=x_codes[:].rearrange("p g l -> p (g l)").bitcast(FP8X4),
-                scales=x_scales[:, 0].rearrange("p g l -> p (g l)"),
-                in_=x_grouped[:].rearrange("p g l j -> p (g l j)"),
-            )
+            middle = slice(PAD * STEP, (PAD + PHASES) * STEP)
+            for g in range(GROUPS):
+                nc.vector.quantize_mx(
+                    out=x_codes[:, g, middle].bitcast(FP8X4),
+                    scales=x_scales[:, 0, g, middle],
+                    in_=x_grouped[:, g].rearrange("p l j -> p (l j)"),
+                )
+            for rows in (codes, scales):
+                nc.vector.tensor_copy(
+                    out=rows[:, :, 0:PAD, 1:STEP], in_=rows[:, :, PHASES : PHASES + PAD, 0 : STEP - 1]
+                )
+                nc.vector.tensor_copy(
+                    out=rows[:, :, PAD + PHASES :, 0 : STEP - 1], in_=rows[:, :, PAD : 2 * PAD, 1:STEP]
+                )
             for plane in range(1, PLANES):
                 nc.vector.tensor_copy(
                     out=x_scales[:, plane, :, 0 : TABLE - plane * STEP].bitcast(I32),

@@ -29,8 +29,10 @@ TURNED = (0, 1)
 REGROUPED = (2, 3)
 HALVES = 2
 HALF_ROWS = ROWS // HALVES
-REGROUPED_RUNS = ((0, 4), (4, 4), (8, 1))
-TURNED_RUNS = ((0, 8), (8, 1))
+HALF_RUNS = ((0, 4), (4, 4))
+LAST_RUN = (8, 1)
+LONG_RUNS = ((0, 8), (8, 1))
+SHORT_RUNS = ((0, 4), (4, 4), (8, 1))
 VECTOR_SEGMENTS = {2: 4, 3: 2}
 STEP = 16
 PHASES = L // STEP
@@ -120,11 +122,10 @@ def tile_partiallyunsharedconv1d_pa_s_kernel(tc, x, weight, conv_bias_param, out
             nc.scalar.copy(out=w_grouped[:, g, TAPS - 1, 0:SEGMENTS:2, :], in_=halves[:, 0:2, 0, :])
             nc.scalar.copy(out=w_grouped[:, g, 0, 1:SEGMENTS:2, :], in_=halves[:, 0:2, 1, :])
 
-        def regroup_weights(g, h):
+        def regroup_weights(g, rows, runs):
             loaded = w_raw[:, g].rearrange("p (r s f) -> p r s f", s=SEGMENTS, f=TAPS)
             split = VECTOR_SEGMENTS[g]
-            rows = slice(h * HALF_ROWS, (h + 1) * HALF_ROWS)
-            for f0, n in REGROUPED_RUNS:
+            for f0, n in runs:
                 taps = slice(f0, f0 + n)
                 nc.vector.tensor_copy(
                     out=w_grouped[:, g, taps, 0:split, rows].rearrange("p f s r -> p s r f"),
@@ -218,21 +219,25 @@ def tile_partiallyunsharedconv1d_pa_s_kernel(tc, x, weight, conv_bias_param, out
 
             t0, t1 = TURNED
             r0, r1 = REGROUPED
+            halves = (slice(0, HALF_ROWS), slice(HALF_ROWS, ROWS))
+            whole = slice(0, ROWS)
             turn_weights(t0)
-            regroup_weights(r0, 0)
-            quantise_weights(t0, TURNED_RUNS)
+            regroup_weights(r0, halves[0], HALF_RUNS)
+            quantise_weights(t0, LONG_RUNS)
             turn_weights(t1)
-            regroup_weights(r0, 1)
-            quantise_weights(r0, REGROUPED_RUNS)
+            regroup_weights(r0, halves[1], HALF_RUNS)
+            regroup_weights(r0, whole, [LAST_RUN])
+            quantise_weights(r0, LONG_RUNS)
             acc_t0 = convolve(t0)
             acc_r0 = convolve(r0)
-            regroup_weights(r1, 0)
+            regroup_weights(r1, halves[0], HALF_RUNS)
             finish(t0, acc_t0)
-            quantise_weights(t1, TURNED_RUNS)
+            quantise_weights(t1, LONG_RUNS)
             acc_t1 = convolve(t1)
             finish(r0, acc_r0)
-            regroup_weights(r1, 1)
+            regroup_weights(r1, halves[1], HALF_RUNS)
+            regroup_weights(r1, whole, [LAST_RUN])
             finish(t1, acc_t1)
-            quantise_weights(r1, REGROUPED_RUNS)
+            quantise_weights(r1, SHORT_RUNS)
             acc_r1 = convolve(r1)
             finish(r1, acc_r1)

@@ -176,7 +176,7 @@ def tile_partiallyunsharedconv1d_pa_s_kernel(tc, x, weight, conv_bias_param, out
                     in_=result[s * CO : (s + 1) * CO, g, positions],
                 )
 
-        with tc.manual_schedule():
+        with tc.manual_schedule(engines={mybir.EngineType.PE}):
             make_identity(nc, identity[:])
             nc.vector.memset(bias_sorted[:], 0.0)
             nc.scalar.copy(

@@ -22,20 +22,21 @@ SEG_START = (0, 26, 52, 78, 128)
 ROWS = CO * PACK
 PAIRS = SEGMENTS * TAPS // 2
 BANK_WORDS = 4
-WORD_RUNS = ((0, 0, 0), (5, 1, 1), (9, 2, 0), (14, 3, 1))
 STRADDLING = (4, 13)
+PARITY_BANKS = ((0, 0), (1, 1), (0, 4), (1, 5))
 
-TURNED = (0, 1)
-REGROUPED = (2, 3)
+TURNED = (0, 1, 2)
+REGROUPED = (3,)
 HALVES = 2
 HALF_ROWS = ROWS // HALVES
 HALF_RUNS = ((0, 4), (4, 4))
 LAST_RUN = (8, 1)
 LONG_RUNS = ((0, 8), (8, 1))
 SHORT_RUNS = ((0, 4), (4, 4), (8, 1))
-VECTOR_SEGMENTS = {2: 4, 3: 2}
+VECTOR_SEGMENTS = {3: 4}
 STEP = 16
 PHASES = L // STEP
+READ_RUN = 4
 TABLE = (PHASES + TAPS - 1) * STEP
 PLANES = 64 // STEP
 
@@ -83,6 +84,9 @@ def tile_partiallyunsharedconv1d_pa_s_kernel(tc, x, weight, conv_bias_param, out
                 in_=w_fours[g, :, channels, :],
             )
 
+        t0, t1, t2 = TURNED
+        (r0,) = REGROUPED
+        load_turned(t0)
         groups = slice(TURNED[0], TURNED[-1] + 1)
         nc.sync.dma_start(
             out=x_raw[:, groups].rearrange("p g j l -> p (g j) l"),
@@ -92,35 +96,35 @@ def tile_partiallyunsharedconv1d_pa_s_kernel(tc, x, weight, conv_bias_param, out
         nc.sync.dma_start(
             out=x_raw[:, groups].rearrange("p g j l -> p g (j l)"), in_=x_fours[:, groups]
         )
-        load_turned(TURNED[0])
-        load_regrouped(REGROUPED[0], 0)
-        load_turned(TURNED[1])
-        load_regrouped(REGROUPED[0], 1)
-        load_regrouped(REGROUPED[1], 0)
-        load_regrouped(REGROUPED[1], 1)
+        load_turned(t1)
+        load_turned(t2)
+        load_regrouped(r0, 0)
+        load_regrouped(r0, 1)
 
-        def turn_weights(g):
+        def turn(g, word_list):
             words = w_raw[:, g].bitcast(F32).rearrange("p (c w) -> p c w", w=PAIRS)
-
-            def turn(word_list):
-                bank = turned.tile([P, BANK_WORDS * P], F32, name="bank")
-                for slot, w in enumerate(word_list):
-                    nc.tensor.transpose(
-                        bank[:, slot * P : (slot + 1) * P], words[:, :, w], identity[:]
-                    )
-                return bank[:].bitcast(BF16).rearrange(
-                    "p (w n e) -> p w e n", w=BANK_WORDS, e=2
+            bank = turned.tile([P, BANK_WORDS * P], F32, name="bank")
+            for slot, w in enumerate(word_list):
+                nc.tensor.transpose(
+                    bank[:, slot * P : (slot + 1) * P], words[:, :, w], identity[:]
                 )
+            return bank[:].bitcast(BF16)
 
-            for w0, s, f0 in WORD_RUNS:
-                halves = turn(range(w0, w0 + BANK_WORDS))
-                target = w_grouped[:, g, f0 : f0 + 2 * BANK_WORDS, s, :].rearrange(
-                    "p (w e) n -> p w e n", e=2
-                )
-                nc.scalar.copy(out=target, in_=halves)
-            halves = turn(STRADDLING)
-            nc.scalar.copy(out=w_grouped[:, g, TAPS - 1, 0:SEGMENTS:2, :], in_=halves[:, 0:2, 0, :])
-            nc.scalar.copy(out=w_grouped[:, g, 0, 1:SEGMENTS:2, :], in_=halves[:, 0:2, 1, :])
+        def turn_straddling(g, copy):
+            halves = turn(g, STRADDLING).rearrange("p (w n e) -> p w e n", w=BANK_WORDS, e=2)
+            copy(out=w_grouped[:, g, TAPS - 1, 0:SEGMENTS:2, :], in_=halves[:, 0:2, 0, :])
+            copy(out=w_grouped[:, g, 0, 1:SEGMENTS:2, :], in_=halves[:, 0:2, 1, :])
+
+        def turn_parity(g, bank_number, copy):
+            parity, f0 = PARITY_BANKS[bank_number]
+            word_list = [
+                (TAPS * s + f) // 2 for f in (f0, f0 + 2) for s in range(parity, SEGMENTS, 2)
+            ]
+            halves = turn(g, word_list).rearrange("p (k a n e) -> p k a e n", k=2, a=2, e=2)
+            target = w_grouped[:, g, f0 : f0 + 4, parity:SEGMENTS:2, :].rearrange(
+                "p (k e) a n -> p k a e n", e=2
+            )
+            copy(out=target, in_=halves)
 
         def regroup_weights(g, rows, runs):
             loaded = w_raw[:, g].rearrange("p (r s f) -> p r s f", s=SEGMENTS, f=TAPS)
@@ -176,27 +180,35 @@ def tile_partiallyunsharedconv1d_pa_s_kernel(tc, x, weight, conv_bias_param, out
                     in_=result[s * CO : (s + 1) * CO, g, positions],
                 )
 
-        with tc.manual_schedule(engines={mybir.EngineType.PE}):
-            make_identity(nc, identity[:])
-            nc.vector.memset(bias_sorted[:], 0.0)
-            nc.scalar.copy(
-                out=bias_sorted[0:GROUPS], in_=bias_rows[:].rearrange("g o s -> g s o")
-            )
-            bias_t = turned.tile([P, BANK_WORDS * P], F32, name="bank")
-            nc.tensor.transpose(
-                bias_t[:, 0:P], bias_sorted[:].rearrange("p s o -> p (s o)"), identity[:]
-            )
-            nc.vector.tensor_copy(out=bias_column[:], in_=bias_t[:, 0:GROUPS])
+        vector = nc.vector.tensor_copy
+        scalar = nc.scalar.copy
+        halves = (slice(0, HALF_ROWS), slice(HALF_ROWS, ROWS))
+        whole = slice(0, ROWS)
 
+        with tc.manual_schedule():
+            make_identity(nc, identity[:])
             codes = x_codes[:].bitcast(I32).rearrange("p g (a q) -> p g a q", q=STEP)
             scales = x_scales[:, 0].rearrange("p g (a q) -> p g a q", q=STEP)
+            nc.vector.memset(bias_sorted[:], 0.0)
             nc.vector.memset(codes[:, :, 0:PAD], 0)
             nc.vector.memset(codes[:, :, PAD + PHASES :], 0)
             nc.vector.memset(x_scales[:, 0].rearrange("p g l -> p (g l)").bitcast(I32), 0)
-            nc.vector.tensor_copy(
-                out=x_grouped[:].rearrange("p g (r q) j -> p g r q j", q=STEP),
-                in_=x_raw[:].rearrange("p g j (q r) -> p g r q j", r=PHASES),
+            nc.scalar.copy(
+                out=bias_sorted[0:GROUPS], in_=bias_rows[:].rearrange("g o s -> g s o")
             )
+
+            turn_straddling(t0, vector)
+            for bank_number in range(4):
+                turn_parity(t0, bank_number, scalar)
+
+            positions = x_raw[:].rearrange("p g j (q r) -> p g j q r", r=PHASES)
+            columns = x_grouped[:].rearrange("p g (r q) j -> p g r q j", q=STEP)
+            for first in range(0, PHASES, READ_RUN):
+                run = slice(first, first + READ_RUN)
+                nc.vector.tensor_copy(
+                    out=columns[:, :, run].rearrange("p g r q j -> p g q j r"),
+                    in_=positions[:, :, :, :, run].rearrange("p g j q r -> p g q j r"),
+                )
             middle = slice(PAD * STEP, (PAD + PHASES) * STEP)
             for g in range(GROUPS):
                 nc.vector.quantize_mx(
@@ -217,27 +229,32 @@ def tile_partiallyunsharedconv1d_pa_s_kernel(tc, x, weight, conv_bias_param, out
                     in_=x_scales[:, 0, :, plane * STEP : TABLE].bitcast(I32),
                 )
 
-            t0, t1 = TURNED
-            r0, r1 = REGROUPED
-            halves = (slice(0, HALF_ROWS), slice(HALF_ROWS, ROWS))
-            whole = slice(0, ROWS)
-            turn_weights(t0)
+            bias_t = turned.tile([P, BANK_WORDS * P], F32, name="bank")
+            nc.tensor.transpose(
+                bias_t[:, 0:P], bias_sorted[:].rearrange("p s o -> p (s o)"), identity[:]
+            )
+            nc.vector.tensor_copy(out=bias_column[:], in_=bias_t[:, 0:GROUPS])
+
+            quantise_weights(t0, SHORT_RUNS)
+            turn_straddling(t1, vector)
+            for bank_number in range(4):
+                turn_parity(t1, bank_number, scalar)
+            quantise_weights(t1, SHORT_RUNS[0:1])
+            turn_straddling(t2, vector)
+            quantise_weights(t1, SHORT_RUNS[1:3])
+            acc_t0 = convolve(t0)
+            turn_parity(t2, 0, scalar)
+            finish(t0, acc_t0)
             regroup_weights(r0, halves[0], HALF_RUNS)
-            quantise_weights(t0, LONG_RUNS)
-            turn_weights(t1)
+            for bank_number in range(1, 4):
+                turn_parity(t2, bank_number, scalar)
+            acc_t1 = convolve(t1)
+            finish(t1, acc_t1)
             regroup_weights(r0, halves[1], HALF_RUNS)
             regroup_weights(r0, whole, [LAST_RUN])
-            quantise_weights(r0, LONG_RUNS)
-            acc_t0 = convolve(t0)
+            quantise_weights(t2, SHORT_RUNS)
+            acc_t2 = convolve(t2)
+            finish(t2, acc_t2)
+            quantise_weights(r0, SHORT_RUNS)
             acc_r0 = convolve(r0)
-            regroup_weights(r1, halves[0], HALF_RUNS)
-            finish(t0, acc_t0)
-            quantise_weights(t1, LONG_RUNS)
-            acc_t1 = convolve(t1)
             finish(r0, acc_r0)
-            regroup_weights(r1, halves[1], HALF_RUNS)
-            regroup_weights(r1, whole, [LAST_RUN])
-            finish(t1, acc_t1)
-            quantise_weights(r1, SHORT_RUNS)
-            acc_r1 = convolve(r1)
-            finish(r1, acc_r1)

@@ -25,15 +25,12 @@ BANK_WORDS = 4
 STRADDLING = (4, 13)
 PARITY_BANKS = ((0, 0), (1, 1), (0, 4), (1, 5))
 
-TURNED = (0, 1, 2)
-REGROUPED = (3,)
-HALVES = 2
-HALF_ROWS = ROWS // HALVES
-HALF_RUNS = ((0, 4), (4, 4))
+TURNED = (0, 1)
+REGROUPED = (2, 3)
+EARLY_RUNS = ((0, 4), (4, 4))
 LAST_RUN = (8, 1)
 LONG_RUNS = ((0, 8), (8, 1))
 SHORT_RUNS = ((0, 4), (4, 4), (8, 1))
-VECTOR_SEGMENTS = {3: 4}
 STEP = 16
 PHASES = L // STEP
 READ_RUN = 4
@@ -55,7 +52,7 @@ def tile_partiallyunsharedconv1d_pa_s_kernel(tc, x, weight, conv_bias_param, out
 
     with tc.tile_pool(name="keep", bufs=1) as keep, tc.psum_pool(
         name="turned", bufs=4
-    ) as turned, tc.psum_pool(name="sums", bufs=GROUPS) as sums:
+    ) as turned, tc.psum_pool(name="sums", bufs=4) as sums:
         x_raw = keep.tile([P, GROUPS, PACK, L], BF16)
         x_grouped = keep.tile([P, GROUPS, L, PACK], BF16, align_bytes=64)
         x_codes = keep.tile([P, GROUPS, TABLE], U32, align_bytes=64)
@@ -77,16 +74,15 @@ def tile_partiallyunsharedconv1d_pa_s_kernel(tc, x, weight, conv_bias_param, out
         def load_turned(g):
             nc.sync.dma_start(out=w_raw[:, g], in_=w_quarters[g])
 
-        def load_regrouped(g, h):
-            channels = slice(h * CO // HALVES, (h + 1) * CO // HALVES)
+        def load_regrouped(g, first, count):
+            channels = slice(first, first + count)
             nc.sync.dma_start(
                 out=w_raw[:, g].rearrange("p (o n) -> p o n", o=CO)[:, channels, :],
                 in_=w_fours[g, :, channels, :],
             )
 
-        t0, t1, t2 = TURNED
-        (r0,) = REGROUPED
-        load_turned(t0)
+        t0, t1 = TURNED
+        r0, r1 = REGROUPED
         groups = slice(TURNED[0], TURNED[-1] + 1)
         nc.sync.dma_start(
             out=x_raw[:, groups].rearrange("p g j l -> p (g j) l"),
@@ -96,10 +92,13 @@ def tile_partiallyunsharedconv1d_pa_s_kernel(tc, x, weight, conv_bias_param, out
         nc.sync.dma_start(
             out=x_raw[:, groups].rearrange("p g j l -> p g (j l)"), in_=x_fours[:, groups]
         )
+        load_turned(t0)
+        load_regrouped(r0, 0, 16)
         load_turned(t1)
-        load_turned(t2)
-        load_regrouped(r0, 0)
-        load_regrouped(r0, 1)
+        load_regrouped(r0, 16, 16)
+        load_regrouped(r1, 0, 16)
+        load_regrouped(r1, 16, 8)
+        load_regrouped(r1, 24, 8)
 
         def turn(g, word_list):
             words = w_raw[:, g].bitcast(F32).rearrange("p (c w) -> p c w", w=PAIRS)
@@ -126,19 +125,20 @@ def tile_partiallyunsharedconv1d_pa_s_kernel(tc, x, weight, conv_bias_param, out
             )
             copy(out=target, in_=halves)
 
-        def regroup_weights(g, rows, runs):
+        def regroup_weights(g, first, count, runs, split):
             loaded = w_raw[:, g].rearrange("p (r s f) -> p r s f", s=SEGMENTS, f=TAPS)
-            split = VECTOR_SEGMENTS[g]
-            for f0, n in runs:
-                taps = slice(f0, f0 + n)
-                nc.vector.tensor_copy(
-                    out=w_grouped[:, g, taps, 0:split, rows].rearrange("p f s r -> p s r f"),
-                    in_=loaded[:, rows, 0:split, taps].rearrange("p r s f -> p s r f"),
-                )
-                if split < SEGMENTS:
-                    nc.scalar.copy(
-                        out=w_grouped[:, g, taps, split:, rows].rearrange("p f s r -> p s r f"),
-                        in_=loaded[:, rows, split:, taps].rearrange("p r s f -> p s r f"),
+            rows = slice(first * PACK, (first + count) * PACK)
+            for copy, segments in (
+                (nc.vector.tensor_copy, slice(0, split)),
+                (nc.scalar.copy, slice(split, SEGMENTS)),
+            ):
+                if segments.start == segments.stop:
+                    continue
+                for f0, n in runs:
+                    taps = slice(f0, f0 + n)
+                    copy(
+                        out=w_grouped[:, g, taps, segments, rows].rearrange("p f s r -> p s r f"),
+                        in_=loaded[:, rows, segments, taps].rearrange("p r s f -> p s r f"),
                     )
 
         def quantise_weights(g, runs):
@@ -182,8 +182,6 @@ def tile_partiallyunsharedconv1d_pa_s_kernel(tc, x, weight, conv_bias_param, out
 
         vector = nc.vector.tensor_copy
         scalar = nc.scalar.copy
-        halves = (slice(0, HALF_ROWS), slice(HALF_ROWS, ROWS))
-        whole = slice(0, ROWS)
 
         with tc.manual_schedule():
             make_identity(nc, identity[:])
@@ -197,18 +195,24 @@ def tile_partiallyunsharedconv1d_pa_s_kernel(tc, x, weight, conv_bias_param, out
                 out=bias_sorted[0:GROUPS], in_=bias_rows[:].rearrange("g o s -> g s o")
             )
 
-            turn_straddling(t0, vector)
-            for bank_number in range(4):
-                turn_parity(t0, bank_number, scalar)
+            bias_t = sums.tile([P, L], F32, name="acc")
+            nc.tensor.transpose(
+                bias_t[:], bias_sorted[:].rearrange("p s o -> p (s o)"), identity[:]
+            )
 
             positions = x_raw[:].rearrange("p g j (q r) -> p g j q r", r=PHASES)
             columns = x_grouped[:].rearrange("p g (r q) j -> p g r q j", q=STEP)
-            for first in range(0, PHASES, READ_RUN):
+
+            def regroup_x(copy, groups, first):
                 run = slice(first, first + READ_RUN)
-                nc.vector.tensor_copy(
-                    out=columns[:, :, run].rearrange("p g r q j -> p g q j r"),
-                    in_=positions[:, :, :, :, run].rearrange("p g j q r -> p g q j r"),
+                copy(
+                    out=columns[:, groups, run].rearrange("p g r q j -> p g q j r"),
+                    in_=positions[:, groups, :, :, run].rearrange("p g j q r -> p g q j r"),
                 )
+
+            regroup_x(vector, slice(0, GROUPS), 0)
+            regroup_x(scalar, slice(0, 2), READ_RUN)
+            regroup_x(vector, slice(2, GROUPS), READ_RUN)
             middle = slice(PAD * STEP, (PAD + PHASES) * STEP)
             for g in range(GROUPS):
                 nc.vector.quantize_mx(
@@ -228,33 +232,35 @@ def tile_partiallyunsharedconv1d_pa_s_kernel(tc, x, weight, conv_bias_param, out
                     out=x_scales[:, plane, :, 0 : TABLE - plane * STEP].bitcast(I32),
                     in_=x_scales[:, 0, :, plane * STEP : TABLE].bitcast(I32),
                 )
-
-            bias_t = turned.tile([P, BANK_WORDS * P], F32, name="bank")
-            nc.tensor.transpose(
-                bias_t[:, 0:P], bias_sorted[:].rearrange("p s o -> p (s o)"), identity[:]
-            )
             nc.vector.tensor_copy(out=bias_column[:], in_=bias_t[:, 0:GROUPS])
 
-            quantise_weights(t0, SHORT_RUNS)
-            turn_straddling(t1, vector)
-            for bank_number in range(4):
-                turn_parity(t1, bank_number, scalar)
-            quantise_weights(t1, SHORT_RUNS[0:1])
-            turn_straddling(t2, vector)
-            quantise_weights(t1, SHORT_RUNS[1:3])
-            acc_t0 = convolve(t0)
-            turn_parity(t2, 0, scalar)
-            finish(t0, acc_t0)
-            regroup_weights(r0, halves[0], HALF_RUNS)
+            turn_straddling(t0, vector)
+            turn_parity(t0, 0, vector)
+            turn_parity(t0, 1, scalar)
+            regroup_weights(r0, 0, 16, EARLY_RUNS, 4)
+            quantise_weights(t0, SHORT_RUNS[0:1])
+            turn_parity(t0, 2, scalar)
+            turn_parity(t0, 3, scalar)
+            turn_straddling(t1, scalar)
+            quantise_weights(t0, SHORT_RUNS[1:])
+            turn_parity(t1, 0, scalar)
+            regroup_weights(r0, 16, 16, EARLY_RUNS, 4)
+            regroup_weights(r0, 0, 32, [LAST_RUN], 4)
             for bank_number in range(1, 4):
-                turn_parity(t2, bank_number, scalar)
-            acc_t1 = convolve(t1)
-            finish(t1, acc_t1)
-            regroup_weights(r0, halves[1], HALF_RUNS)
-            regroup_weights(r0, whole, [LAST_RUN])
-            quantise_weights(t2, SHORT_RUNS)
-            acc_t2 = convolve(t2)
-            finish(t2, acc_t2)
-            quantise_weights(r0, SHORT_RUNS)
+                turn_parity(t1, bank_number, scalar)
+            quantise_weights(r0, LONG_RUNS)
+            regroup_weights(r1, 0, 16, EARLY_RUNS, 3)
+            acc_t0 = convolve(t0)
             acc_r0 = convolve(r0)
+            quantise_weights(t1, SHORT_RUNS[0:1])
+            finish(t0, acc_t0)
             finish(r0, acc_r0)
+            quantise_weights(t1, SHORT_RUNS[1:])
+            acc_t1 = convolve(t1)
+            regroup_weights(r1, 16, 8, EARLY_RUNS, 3)
+            regroup_weights(r1, 24, 8, EARLY_RUNS, 2)
+            regroup_weights(r1, 0, 32, [LAST_RUN], 3)
+            finish(t1, acc_t1)
+            quantise_weights(r1, SHORT_RUNS)
+            acc_r1 = convolve(r1)
+            finish(r1, acc_r1)

@@ -27,8 +27,11 @@ PARITY_BANKS = ((0, 0), (1, 1), (0, 4), (1, 5))
 
 TURNED = (0, 1)
 REGROUPED = (2, 3)
-EARLY_RUNS = ((0, 4), (4, 4))
-LAST_RUN = (8, 1)
+HALVES = 2
+HALF = CO // HALVES
+HALF_ROWS = HALF * PACK
+HALF_COLUMNS = SEGMENTS * HALF
+REGROUP_RUNS = ((0, 3), (3, 3), (6, 3))
 LONG_RUNS = ((0, 8), (8, 1))
 SHORT_RUNS = ((0, 4), (4, 4), (8, 1))
 STEP = 16
@@ -43,7 +46,6 @@ FLOPS = 2 * GROUPS * CO * L * CI * TAPS
 def tile_partiallyunsharedconv1d_pa_s_kernel(tc, x, weight, conv_bias_param, out):
     nc = tc.nc
 
-    x_quarters = x.rearrange("b d k (j p) l -> p (b d k) j l", p=P)
     x_fours = x.rearrange("b d k (p j) l -> p (b d k) (j l)", j=PACK)
     w_quarters = weight.rearrange("d k o (j c) s u f -> (d k) (o j) (c s u f)", j=PACK)
     w_fours = weight.rearrange("d k o (p j) s u f -> (d k) p o (j s u f)", j=PACK)
@@ -63,10 +65,18 @@ def tile_partiallyunsharedconv1d_pa_s_kernel(tc, x, weight, conv_bias_param, out
         w_codes = keep.tile([P, GROUPS, TAPS, SEGMENTS * CO], U32, align_bytes=64)
         w_scales = keep.tile([P, GROUPS, TAPS, SEGMENTS * CO], U8, align_bytes=64)
 
+        h_grouped = keep.tile([P, HALVES, TAPS, SEGMENTS, HALF_ROWS], BF16, align_bytes=64)
+        h_codes = keep.tile([P, HALVES * TAPS + 1, HALF_COLUMNS], U32, align_bytes=64)
+        h_scales = keep.tile([P, HALVES * TAPS + 1, HALF_COLUMNS], U8, align_bytes=64)
+
         bias_rows = keep.tile([GROUPS, CO, SEGMENTS], BF16)
         bias_sorted = keep.tile([P, SEGMENTS, CO], F32)
         bias_column = keep.tile([P, GROUPS], F32)
+        bias_by_half = keep.tile([P, HALVES, SEGMENTS, HALF], F32)
+        bias_half_column = keep.tile([P, 1], F32)
         identity = keep.tile([P, P], F32)
+        identity_bf16 = keep.tile([P, P], BF16)
+        x_turned = keep.tile([P, len(TURNED), CI], BF16)
         result = keep.tile([P, GROUPS, L], F32)
 
         nc.sync.dma_start(out=bias_rows[:].rearrange("g o s -> g (o s)"), in_=bias_view)
@@ -83,19 +93,16 @@ def tile_partiallyunsharedconv1d_pa_s_kernel(tc, x, weight, conv_bias_param, out
 
         t0, t1 = TURNED
         r0, r1 = REGROUPED
-        groups = slice(TURNED[0], TURNED[-1] + 1)
-        nc.sync.dma_start(
-            out=x_raw[:, groups].rearrange("p g j l -> p (g j) l"),
-            in_=x_quarters[:, groups].rearrange("p g j l -> p (g j) l"),
-        )
-        groups = slice(REGROUPED[0], REGROUPED[-1] + 1)
-        nc.sync.dma_start(
-            out=x_raw[:, groups].rearrange("p g j l -> p g (j l)"), in_=x_fours[:, groups]
-        )
+        for road in (TURNED, REGROUPED):
+            groups = slice(road[0], road[-1] + 1)
+            nc.sync.dma_start(
+                out=x_raw[:, groups].rearrange("p g j l -> p g (j l)"), in_=x_fours[:, groups]
+            )
         load_turned(t0)
         load_regrouped(r0, 0, 16)
         load_turned(t1)
-        load_regrouped(r0, 16, 16)
+        load_regrouped(r0, 16, 8)
+        load_regrouped(r0, 24, 8)
         load_regrouped(r1, 0, 16)
         load_regrouped(r1, 16, 8)
         load_regrouped(r1, 24, 8)
@@ -125,21 +132,21 @@ def tile_partiallyunsharedconv1d_pa_s_kernel(tc, x, weight, conv_bias_param, out
             )
             copy(out=target, in_=halves)
 
-        def regroup_weights(g, first, count, runs, split):
-            loaded = w_raw[:, g].rearrange("p (r s f) -> p r s f", s=SEGMENTS, f=TAPS)
+        def regroup_weights(copy, g, first, count, runs=REGROUP_RUNS):
+            target = w_grouped[:, g]
             rows = slice(first * PACK, (first + count) * PACK)
-            for copy, segments in (
-                (nc.vector.tensor_copy, slice(0, split)),
-                (nc.scalar.copy, slice(split, SEGMENTS)),
-            ):
-                if segments.start == segments.stop:
-                    continue
-                for f0, n in runs:
-                    taps = slice(f0, f0 + n)
-                    copy(
-                        out=w_grouped[:, g, taps, segments, rows].rearrange("p f s r -> p s r f"),
-                        in_=loaded[:, rows, segments, taps].rearrange("p r s f -> p s r f"),
-                    )
+            out_rows = rows
+            if g == REGROUPED[-1]:
+                half, inside = divmod(first, HALF)
+                target = h_grouped[:, half]
+                out_rows = slice(inside * PACK, (inside + count) * PACK)
+            loaded = w_raw[:, g].rearrange("p (r s f) -> p r s f", s=SEGMENTS, f=TAPS)
+            for f0, n in runs:
+                taps = slice(f0, f0 + n)
+                copy(
+                    out=target[:, taps, :, out_rows].rearrange("p f s r -> p s r f"),
+                    in_=loaded[:, rows, :, taps].rearrange("p r s f -> p s r f"),
+                )
 
         def quantise_weights(g, runs):
             for f0, n in runs:
@@ -148,6 +155,52 @@ def tile_partiallyunsharedconv1d_pa_s_kernel(tc, x, weight, conv_bias_param, out
                     out=w_codes[:, g, taps].rearrange("p f n -> p (f n)").bitcast(FP8X4),
                     scales=w_scales[:, g, taps].rearrange("p f n -> p (f n)"),
                     in_=w_grouped[:, g, taps].rearrange("p f s n -> p (f s n)"),
+                )
+
+        def quantise_half(half, runs):
+            first = half * (TAPS + 1)
+            for f0, n in runs:
+                taps = slice(first + f0, first + f0 + n)
+                nc.vector.quantize_mx(
+                    out=h_codes[:, taps].rearrange("p f n -> p (f n)").bitcast(FP8X4),
+                    scales=h_scales[:, taps].rearrange("p f n -> p (f n)"),
+                    in_=h_grouped[:, half, f0 : f0 + n].rearrange("p f s n -> p (f s n)"),
+                )
+
+        def convolve_half(half):
+            acc = sums.tile([P, L], F32, name="acc")
+            g = REGROUPED[-1]
+            codes = h_codes[:].rearrange("p f n -> p (f n)")
+            scales = h_scales[:].rearrange("p f n -> p (f n)")
+            for f in range(TAPS):
+                plane = f % PLANES
+                start = (half * TAPS + f) * HALF_COLUMNS
+                nc.tensor.matmul_mx(
+                    out=acc[:],
+                    lhsT=codes[:, start : start + P].bitcast(FP8X4),
+                    lhsT_scale=scales[:, start : start + P],
+                    rhs=x_codes[:, g, f * STEP : f * STEP + L].bitcast(FP8X4),
+                    rhs_scale=x_scales[:, plane, g, (f - plane) * STEP : (f - plane) * STEP + L],
+                    start=(f == 0),
+                    stop=(f == TAPS - 1),
+                )
+            return acc
+
+        def finish_half(half, acc):
+            g = REGROUPED[-1]
+            rows = slice(half * HALF_COLUMNS, (half + 1) * HALF_COLUMNS)
+            nc.scalar.activation(
+                out=result[rows, g, :].rearrange("p (q r) -> p q r", r=PHASES),
+                in_=acc[rows].rearrange("p (r q) -> p q r", q=STEP),
+                func=mybir.ActivationFunctionType.Identity,
+                bias=bias_half_column[rows],
+            )
+            for s in range(SEGMENTS):
+                positions = slice(SEG_START[s], SEG_START[s + 1])
+                first = half * HALF_COLUMNS + s * HALF
+                nc.sync.dma_start(
+                    out=out_view[g, half * HALF : (half + 1) * HALF, positions],
+                    in_=result[first : first + HALF, g, positions],
                 )
 
         def convolve(g):
@@ -185,36 +238,67 @@ def tile_partiallyunsharedconv1d_pa_s_kernel(tc, x, weight, conv_bias_param, out
 
         with tc.manual_schedule():
             make_identity(nc, identity[:])
+            nc.vector.tensor_copy(out=identity_bf16[:], in_=identity[:])
             codes = x_codes[:].bitcast(I32).rearrange("p g (a q) -> p g a q", q=STEP)
             scales = x_scales[:, 0].rearrange("p g (a q) -> p g a q", q=STEP)
             nc.vector.memset(bias_sorted[:], 0.0)
+            nc.vector.memset(bias_by_half[:], 0.0)
+            nc.vector.memset(h_codes[:, TAPS].bitcast(I32), 0)
+            nc.vector.memset(h_scales[:, TAPS].bitcast(I32), 0)
             nc.vector.memset(codes[:, :, 0:PAD], 0)
             nc.vector.memset(codes[:, :, PAD + PHASES :], 0)
             nc.vector.memset(x_scales[:, 0].rearrange("p g l -> p (g l)").bitcast(I32), 0)
             nc.scalar.copy(
                 out=bias_sorted[0:GROUPS], in_=bias_rows[:].rearrange("g o s -> g s o")
             )
+            nc.scalar.copy(
+                out=bias_by_half[0:GROUPS],
+                in_=bias_rows[:].rearrange("g (h o) s -> g h s o", h=HALVES),
+            )
+
+            columns = x_grouped[:].rearrange("p g (r q) j -> p g r q j", q=STEP)
+
+            def transpose_x(parts):
+                bank = turned.tile([P, BANK_WORDS * P], F32, name="bank")
+                halves = bank[:].bitcast(BF16)[:, 0 : PACK * P]
+                for j, part in enumerate(parts):
+                    nc.tensor.transpose(halves[:, j * P : (j + 1) * P], part, identity_bf16[:])
+                return halves
+
+            for g in TURNED:
+                by_position = transpose_x([x_raw[:, g, j, :] for j in range(PACK)])
+                nc.scalar.copy(
+                    out=x_turned[:, g].rearrange("l (p j) -> l p j", j=PACK),
+                    in_=by_position.rearrange("l (j p) -> l p j", j=PACK),
+                )
 
             bias_t = sums.tile([P, L], F32, name="acc")
             nc.tensor.transpose(
                 bias_t[:], bias_sorted[:].rearrange("p s o -> p (s o)"), identity[:]
             )
+            bias_half_t = sums.tile([P, L], F32, name="acc")
+            nc.tensor.transpose(
+                bias_half_t[:], bias_by_half[:].rearrange("p h s o -> p (h s o)"), identity[:]
+            )
+
+            for g in TURNED:
+                by_channel = transpose_x(
+                    [x_turned[:, g, j * P : (j + 1) * P] for j in range(PACK)]
+                )
+                nc.scalar.copy(
+                    out=columns[:, g], in_=by_channel.rearrange("p (j q r) -> p r q j", j=PACK, r=PHASES)
+                )
 
             positions = x_raw[:].rearrange("p g j (q r) -> p g j q r", r=PHASES)
-            columns = x_grouped[:].rearrange("p g (r q) j -> p g r q j", q=STEP)
-
-            def regroup_x(copy, groups, first):
+            groups = slice(REGROUPED[0], REGROUPED[-1] + 1)
+            for first in range(0, PHASES, READ_RUN):
                 run = slice(first, first + READ_RUN)
-                copy(
+                nc.vector.tensor_copy(
                     out=columns[:, groups, run].rearrange("p g r q j -> p g q j r"),
                     in_=positions[:, groups, :, :, run].rearrange("p g j q r -> p g q j r"),
                 )
-
-            regroup_x(vector, slice(0, GROUPS), 0)
-            regroup_x(scalar, slice(0, 2), READ_RUN)
-            regroup_x(vector, slice(2, GROUPS), READ_RUN)
             middle = slice(PAD * STEP, (PAD + PHASES) * STEP)
-            for g in range(GROUPS):
+            for g in REGROUPED + TURNED:
                 nc.vector.quantize_mx(
                     out=x_codes[:, g, middle].bitcast(FP8X4),
                     scales=x_scales[:, 0, g, middle],
@@ -233,34 +317,42 @@ def tile_partiallyunsharedconv1d_pa_s_kernel(tc, x, weight, conv_bias_param, out
                     in_=x_scales[:, 0, :, plane * STEP : TABLE].bitcast(I32),
                 )
             nc.vector.tensor_copy(out=bias_column[:], in_=bias_t[:, 0:GROUPS])
+            nc.vector.tensor_copy(
+                out=bias_half_column[:], in_=bias_half_t[:, REGROUPED[-1] : REGROUPED[-1] + 1]
+            )
 
-            turn_straddling(t0, vector)
-            turn_parity(t0, 0, vector)
+            turn_straddling(t0, scalar)
+            turn_parity(t0, 0, scalar)
             turn_parity(t0, 1, scalar)
-            regroup_weights(r0, 0, 16, EARLY_RUNS, 4)
+            regroup_weights(vector, r0, 0, 16)
             quantise_weights(t0, SHORT_RUNS[0:1])
             turn_parity(t0, 2, scalar)
-            turn_parity(t0, 3, scalar)
-            turn_straddling(t1, scalar)
+            turn_parity(t0, 3, vector)
             quantise_weights(t0, SHORT_RUNS[1:])
+            turn_straddling(t1, scalar)
+            regroup_weights(vector, r0, 16, 8)
             turn_parity(t1, 0, scalar)
-            regroup_weights(r0, 16, 16, EARLY_RUNS, 4)
-            regroup_weights(r0, 0, 32, [LAST_RUN], 4)
-            for bank_number in range(1, 4):
-                turn_parity(t1, bank_number, scalar)
-            quantise_weights(r0, LONG_RUNS)
-            regroup_weights(r1, 0, 16, EARLY_RUNS, 3)
+            turn_parity(t1, 1, scalar)
+            regroup_weights(vector, r0, 24, 8)
+            turn_parity(t1, 2, scalar)
+            turn_parity(t1, 3, scalar)
             acc_t0 = convolve(t0)
-            acc_r0 = convolve(r0)
-            quantise_weights(t1, SHORT_RUNS[0:1])
             finish(t0, acc_t0)
-            finish(r0, acc_r0)
-            quantise_weights(t1, SHORT_RUNS[1:])
+            quantise_weights(r0, LONG_RUNS)
+            acc_r0 = convolve(r0)
+            regroup_weights(vector, r1, 0, 16, REGROUP_RUNS[0:2])
+            regroup_weights(scalar, r1, 0, 16, REGROUP_RUNS[2:3])
+            quantise_weights(t1, SHORT_RUNS)
+            quantise_half(0, LONG_RUNS)
             acc_t1 = convolve(t1)
-            regroup_weights(r1, 16, 8, EARLY_RUNS, 3)
-            regroup_weights(r1, 24, 8, EARLY_RUNS, 2)
-            regroup_weights(r1, 0, 32, [LAST_RUN], 3)
+            acc_0 = convolve_half(0)
+            regroup_weights(vector, r1, 16, 8, REGROUP_RUNS[0:1])
+            regroup_weights(scalar, r1, 16, 8, REGROUP_RUNS[1:3])
+            finish(r0, acc_r0)
+            regroup_weights(vector, r1, 24, 8, REGROUP_RUNS[0:2])
+            regroup_weights(scalar, r1, 24, 8, REGROUP_RUNS[2:3])
             finish(t1, acc_t1)
-            quantise_weights(r1, SHORT_RUNS)
-            acc_r1 = convolve(r1)
-            finish(r1, acc_r1)
+            finish_half(0, acc_0)
+            quantise_half(1, SHORT_RUNS)
+            acc_1 = convolve_half(1)
+            finish_half(1, acc_1)

@@ -54,7 +54,9 @@ def tile_partiallyunsharedconv1d_pa_s_kernel(tc, x, weight, conv_bias_param, out
 
     with tc.tile_pool(name="keep", bufs=1) as keep, tc.psum_pool(
         name="turned", bufs=4
-    ) as turned, tc.psum_pool(name="sums", bufs=4) as sums:
+    ) as turned, tc.psum_pool(name="sums", bufs=3) as sums, tc.psum_pool(
+        name="spare", bufs=1
+    ) as spare:
         x_raw = keep.tile([P, GROUPS, PACK, L], BF16)
         x_grouped = keep.tile([P, GROUPS, L, PACK], BF16, align_bytes=64)
         x_codes = keep.tile([P, GROUPS, TABLE], U32, align_bytes=64)
@@ -71,6 +73,7 @@ def tile_partiallyunsharedconv1d_pa_s_kernel(tc, x, weight, conv_bias_param, out
 
         bias_rows = keep.tile([GROUPS, CO, SEGMENTS], BF16)
         bias_sorted = keep.tile([P, SEGMENTS, CO], F32)
+        table_loaded = keep.tile([P, 1], F32)
         bias_column = keep.tile([P, GROUPS], F32)
         bias_by_half = keep.tile([P, HALVES, SEGMENTS, HALF], F32)
         bias_half_column = keep.tile([P, 1], F32)
@@ -79,7 +82,6 @@ def tile_partiallyunsharedconv1d_pa_s_kernel(tc, x, weight, conv_bias_param, out
         x_turned = keep.tile([P, len(TURNED), CI], BF16)
         result = keep.tile([P, GROUPS, L], F32)
 
-        nc.sync.dma_start(out=bias_rows[:].rearrange("g o s -> g (o s)"), in_=bias_view)
 
         def load_turned(g):
             nc.sync.dma_start(out=w_raw[:, g], in_=w_quarters[g])
@@ -99,6 +101,7 @@ def tile_partiallyunsharedconv1d_pa_s_kernel(tc, x, weight, conv_bias_param, out
                 out=x_raw[:, groups].rearrange("p g j l -> p g (j l)"), in_=x_fours[:, groups]
             )
         load_turned(t0)
+        nc.sync.dma_start(out=bias_rows[:].rearrange("g o s -> g (o s)"), in_=bias_view)
         load_regrouped(r0, 0, 16)
         load_turned(t1)
         load_regrouped(r0, 16, 8)
@@ -155,6 +158,20 @@ def tile_partiallyunsharedconv1d_pa_s_kernel(tc, x, weight, conv_bias_param, out
                     out=w_codes[:, g, taps].rearrange("p f n -> p (f n)").bitcast(FP8X4),
                     scales=w_scales[:, g, taps].rearrange("p f n -> p (f n)"),
                     in_=w_grouped[:, g, taps].rearrange("p f s n -> p (f s n)"),
+                )
+
+        unread = spare.tile([P, 2 * L], F32)
+
+        def keep_warm(count):
+            for i in range(count):
+                nc.tensor.matmul_mx(
+                    out=unread[:],
+                    lhsT=w_codes[:, t0, 0].bitcast(FP8X4),
+                    lhsT_scale=w_scales[:, t0, 0],
+                    rhs=x_codes[:, t0].bitcast(FP8X4),
+                    rhs_scale=x_scales[:, 0, t0],
+                    start=True,
+                    stop=True,
                 )
 
         def quantise_half(half, runs):
@@ -248,12 +265,10 @@ def tile_partiallyunsharedconv1d_pa_s_kernel(tc, x, weight, conv_bias_param, out
             nc.vector.memset(codes[:, :, 0:PAD], 0)
             nc.vector.memset(codes[:, :, PAD + PHASES :], 0)
             nc.vector.memset(x_scales[:, 0].rearrange("p g l -> p (g l)").bitcast(I32), 0)
-            nc.scalar.copy(
-                out=bias_sorted[0:GROUPS], in_=bias_rows[:].rearrange("g o s -> g s o")
-            )
-            nc.scalar.copy(
-                out=bias_by_half[0:GROUPS],
-                in_=bias_rows[:].rearrange("g (h o) s -> g h s o", h=HALVES),
+            nc.scalar.activation(
+                out=table_loaded[:],
+                in_=identity[:, 0:1],
+                func=mybir.ActivationFunctionType.Identity,
             )
 
             columns = x_grouped[:].rearrange("p g (r q) j -> p g r q j", q=STEP)
@@ -271,15 +286,6 @@ def tile_partiallyunsharedconv1d_pa_s_kernel(tc, x, weight, conv_bias_param, out
                     out=x_turned[:, g].rearrange("l (p j) -> l p j", j=PACK),
                     in_=by_position.rearrange("l (j p) -> l p j", j=PACK),
                 )
-
-            bias_t = sums.tile([P, L], F32, name="acc")
-            nc.tensor.transpose(
-                bias_t[:], bias_sorted[:].rearrange("p s o -> p (s o)"), identity[:]
-            )
-            bias_half_t = sums.tile([P, L], F32, name="acc")
-            nc.tensor.transpose(
-                bias_half_t[:], bias_by_half[:].rearrange("p h s o -> p (h s o)"), identity[:]
-            )
 
             for g in TURNED:
                 by_channel = transpose_x(
@@ -316,19 +322,34 @@ def tile_partiallyunsharedconv1d_pa_s_kernel(tc, x, weight, conv_bias_param, out
                     out=x_scales[:, plane, :, 0 : TABLE - plane * STEP].bitcast(I32),
                     in_=x_scales[:, 0, :, plane * STEP : TABLE].bitcast(I32),
                 )
-            nc.vector.tensor_copy(out=bias_column[:], in_=bias_t[:, 0:GROUPS])
-            nc.vector.tensor_copy(
-                out=bias_half_column[:], in_=bias_half_t[:, REGROUPED[-1] : REGROUPED[-1] + 1]
-            )
 
             turn_straddling(t0, scalar)
+            nc.scalar.copy(
+                out=bias_sorted[0:GROUPS], in_=bias_rows[:].rearrange("g o s -> g s o")
+            )
+            nc.scalar.copy(
+                out=bias_by_half[0:GROUPS],
+                in_=bias_rows[:].rearrange("g (h o) s -> g h s o", h=HALVES),
+            )
             turn_parity(t0, 0, scalar)
             turn_parity(t0, 1, scalar)
             regroup_weights(vector, r0, 0, 16)
             quantise_weights(t0, SHORT_RUNS[0:1])
             turn_parity(t0, 2, scalar)
             turn_parity(t0, 3, vector)
+            bias_t = sums.tile([P, L], F32, name="acc")
+            nc.tensor.transpose(
+                bias_t[:], bias_sorted[:].rearrange("p s o -> p (s o)"), identity[:]
+            )
+            bias_half_t = sums.tile([P, L], F32, name="acc")
+            nc.tensor.transpose(
+                bias_half_t[:], bias_by_half[:].rearrange("p h s o -> p (h s o)"), identity[:]
+            )
             quantise_weights(t0, SHORT_RUNS[1:])
+            nc.vector.tensor_copy(out=bias_column[:], in_=bias_t[:, 0:GROUPS])
+            nc.vector.tensor_copy(
+                out=bias_half_column[:], in_=bias_half_t[:, REGROUPED[-1] : REGROUPED[-1] + 1]
+            )
             turn_straddling(t1, scalar)
             regroup_weights(vector, r0, 16, 8)
             turn_parity(t1, 0, scalar)
@@ -340,18 +361,20 @@ def tile_partiallyunsharedconv1d_pa_s_kernel(tc, x, weight, conv_bias_param, out
             finish(t0, acc_t0)
             quantise_weights(r0, LONG_RUNS)
             acc_r0 = convolve(r0)
+            finish(r0, acc_r0)
+            keep_warm(4)
+            quantise_weights(t1, SHORT_RUNS[0:1])
             regroup_weights(vector, r1, 0, 16, REGROUP_RUNS[0:2])
             regroup_weights(scalar, r1, 0, 16, REGROUP_RUNS[2:3])
-            quantise_weights(t1, SHORT_RUNS)
+            quantise_weights(t1, SHORT_RUNS[1:])
             quantise_half(0, LONG_RUNS)
             acc_t1 = convolve(t1)
             acc_0 = convolve_half(0)
-            regroup_weights(vector, r1, 16, 8, REGROUP_RUNS[0:1])
-            regroup_weights(scalar, r1, 16, 8, REGROUP_RUNS[1:3])
-            finish(r0, acc_r0)
+            keep_warm(3)
+            regroup_weights(scalar, r1, 16, 8)
+            finish(t1, acc_t1)
             regroup_weights(vector, r1, 24, 8, REGROUP_RUNS[0:2])
             regroup_weights(scalar, r1, 24, 8, REGROUP_RUNS[2:3])
-            finish(t1, acc_t1)
             finish_half(0, acc_0)
             quantise_half(1, SHORT_RUNS)
             acc_1 = convolve_half(1)

@@ -54,9 +54,7 @@ def tile_partiallyunsharedconv1d_pa_s_kernel(tc, x, weight, conv_bias_param, out
 
     with tc.tile_pool(name="keep", bufs=1) as keep, tc.psum_pool(
         name="turned", bufs=4
-    ) as turned, tc.psum_pool(name="sums", bufs=3) as sums, tc.psum_pool(
-        name="spare", bufs=1
-    ) as spare:
+    ) as turned, tc.psum_pool(name="sums", bufs=4) as sums:
         x_raw = keep.tile([P, GROUPS, PACK, L], BF16)
         x_grouped = keep.tile([P, GROUPS, L, PACK], BF16, align_bytes=64)
         x_codes = keep.tile([P, GROUPS, TABLE], U32, align_bytes=64)
@@ -107,8 +105,8 @@ def tile_partiallyunsharedconv1d_pa_s_kernel(tc, x, weight, conv_bias_param, out
         load_regrouped(r0, 16, 8)
         load_regrouped(r0, 24, 8)
         load_regrouped(r1, 0, 16)
-        load_regrouped(r1, 16, 8)
-        load_regrouped(r1, 24, 8)
+        load_regrouped(r1, 16, 12)
+        load_regrouped(r1, 28, 4)
 
         def turn(g, word_list):
             words = w_raw[:, g].bitcast(F32).rearrange("p (c w) -> p c w", w=PAIRS)
@@ -158,20 +156,6 @@ def tile_partiallyunsharedconv1d_pa_s_kernel(tc, x, weight, conv_bias_param, out
                     out=w_codes[:, g, taps].rearrange("p f n -> p (f n)").bitcast(FP8X4),
                     scales=w_scales[:, g, taps].rearrange("p f n -> p (f n)"),
                     in_=w_grouped[:, g, taps].rearrange("p f s n -> p (f s n)"),
-                )
-
-        unread = spare.tile([P, 2 * L], F32)
-
-        def keep_warm(count):
-            for i in range(count):
-                nc.tensor.matmul_mx(
-                    out=unread[:],
-                    lhsT=w_codes[:, t0, 0].bitcast(FP8X4),
-                    lhsT_scale=w_scales[:, t0, 0],
-                    rhs=x_codes[:, t0].bitcast(FP8X4),
-                    rhs_scale=x_scales[:, 0, t0],
-                    start=True,
-                    stop=True,
                 )
 
         def quantise_half(half, runs):
@@ -235,7 +219,7 @@ def tile_partiallyunsharedconv1d_pa_s_kernel(tc, x, weight, conv_bias_param, out
                 )
             return acc
 
-        def finish(g, acc):
+        def fetch(g, acc):
             nc.scalar.activation(
                 out=result[:, g, :].rearrange("p (q r) -> p q r", r=PHASES),
                 in_=acc[:].rearrange("p (r q) -> p q r", q=STEP),
@@ -243,11 +227,12 @@ def tile_partiallyunsharedconv1d_pa_s_kernel(tc, x, weight, conv_bias_param, out
                 bias=bias_column[:, g : g + 1],
             )
 
+        def store(groups):
             for s in range(SEGMENTS):
                 positions = slice(SEG_START[s], SEG_START[s + 1])
                 nc.sync.dma_start(
-                    out=out_view[g, :, positions],
-                    in_=result[s * CO : (s + 1) * CO, g, positions],
+                    out=out_view[groups, :, positions].rearrange("g o l -> o g l"),
+                    in_=result[s * CO : (s + 1) * CO, groups, positions],
                 )
 
         vector = nc.vector.tensor_copy
@@ -358,23 +343,23 @@ def tile_partiallyunsharedconv1d_pa_s_kernel(tc, x, weight, conv_bias_param, out
             turn_parity(t1, 2, scalar)
             turn_parity(t1, 3, scalar)
             acc_t0 = convolve(t0)
-            finish(t0, acc_t0)
+            fetch(t0, acc_t0)
             quantise_weights(r0, LONG_RUNS)
             acc_r0 = convolve(r0)
-            finish(r0, acc_r0)
-            keep_warm(4)
-            quantise_weights(t1, SHORT_RUNS[0:1])
             regroup_weights(vector, r1, 0, 16, REGROUP_RUNS[0:2])
             regroup_weights(scalar, r1, 0, 16, REGROUP_RUNS[2:3])
-            quantise_weights(t1, SHORT_RUNS[1:])
+            fetch(r0, acc_r0)
+            store(slice(t0, r0 + 1, r0 - t0))
+            quantise_weights(t1, SHORT_RUNS)
             quantise_half(0, LONG_RUNS)
             acc_t1 = convolve(t1)
             acc_0 = convolve_half(0)
-            keep_warm(3)
-            regroup_weights(scalar, r1, 16, 8)
-            finish(t1, acc_t1)
-            regroup_weights(vector, r1, 24, 8, REGROUP_RUNS[0:2])
-            regroup_weights(scalar, r1, 24, 8, REGROUP_RUNS[2:3])
+            regroup_weights(vector, r1, 16, 12, REGROUP_RUNS[0:1])
+            regroup_weights(scalar, r1, 16, 12, REGROUP_RUNS[1:3])
+            regroup_weights(vector, r1, 28, 4, REGROUP_RUNS[0:2])
+            regroup_weights(scalar, r1, 28, 4, REGROUP_RUNS[2:3])
+            fetch(t1, acc_t1)
+            store(slice(t1, t1 + 1))
             finish_half(0, acc_0)
             quantise_half(1, SHORT_RUNS)
             acc_1 = convolve_half(1)

import concourse.mybir as mybir
from concourse.masks import make_identity

BF16 = mybir.dt.bfloat16
F32 = mybir.dt.float32
U32 = mybir.dt.uint32
U8 = mybir.dt.uint8
I32 = mybir.dt.int32
FP8X4 = mybir.dt.float8_e4m3fn_x4

P = 128
PACK = 4
GROUPS = 4
CI = 512
CO = 32
L = 128
SEGMENTS = 4
TAPS = 9
PAD = 4
SEG_START = (0, 26, 52, 78, 128)

ROWS = CO * PACK
PAIRS = SEGMENTS * TAPS // 2
BANK_WORDS = 4
STRADDLING = (4, 13)
PARITY_BANKS = ((0, 0), (1, 1), (0, 4), (1, 5))

TURNED = (0, 1)
REGROUPED = (2, 3)
HALVES = 2
HALF = CO // HALVES
HALF_ROWS = HALF * PACK
HALF_COLUMNS = SEGMENTS * HALF
REGROUP_RUNS = ((0, 3), (3, 3), (6, 3))
LONG_RUNS = ((0, 8), (8, 1))
SHORT_RUNS = ((0, 4), (4, 4), (8, 1))
STEP = 16
PHASES = L // STEP
READ_RUN = 4
TABLE = (PHASES + TAPS - 1) * STEP
PLANES = 64 // STEP

FLOPS = 2 * GROUPS * CO * L * CI * TAPS


def tile_partiallyunsharedconv1d_pa_s_kernel(tc, x, weight, conv_bias_param, out):
    nc = tc.nc

    x_fours = x.rearrange("b d k (p j) l -> p (b d k) (j l)", j=PACK)
    w_quarters = weight.rearrange("d k o (j c) s u f -> (d k) (o j) (c s u f)", j=PACK)
    w_fours = weight.rearrange("d k o (p j) s u f -> (d k) p o (j s u f)", j=PACK)
    bias_view = conv_bias_param.rearrange("d k o s u -> (d k) (o s u)")
    out_view = out.rearrange("b d k o l -> (b d k) o l")

    with tc.tile_pool(name="keep", bufs=1) as keep, tc.psum_pool(
        name="turned", bufs=4
    ) as turned, tc.psum_pool(name="sums", bufs=4) as sums:
        x_raw = keep.tile([P, GROUPS, PACK, L], BF16)
        x_grouped = keep.tile([P, GROUPS, L, PACK], BF16, align_bytes=64)
        x_codes = keep.tile([P, GROUPS, TABLE], U32, align_bytes=64)
        x_scales = keep.tile([P, PLANES, GROUPS, TABLE], U8, align_bytes=64)

        w_raw = keep.tile([P, GROUPS, ROWS * SEGMENTS * TAPS], BF16)
        w_grouped = keep.tile([P, GROUPS, TAPS, SEGMENTS, ROWS], BF16, align_bytes=64)
        w_codes = keep.tile([P, GROUPS, TAPS, SEGMENTS * CO], U32, align_bytes=64)
        w_scales = keep.tile([P, GROUPS, TAPS, SEGMENTS * CO], U8, align_bytes=64)

        h_grouped = keep.tile([P, HALVES, TAPS, SEGMENTS, HALF_ROWS], BF16, align_bytes=64)
        h_codes = keep.tile([P, HALVES * TAPS + 1, HALF_COLUMNS], U32, align_bytes=64)
        h_scales = keep.tile([P, HALVES * TAPS + 1, HALF_COLUMNS], U8, align_bytes=64)

        bias_rows = keep.tile([GROUPS, CO, SEGMENTS], BF16)
        bias_sorted = keep.tile([P, SEGMENTS, CO], F32)
        table_loaded = keep.tile([P, 1], F32)
        bias_column = keep.tile([P, GROUPS], F32)
        bias_by_half = keep.tile([P, HALVES, SEGMENTS, HALF], F32)
        bias_half_column = keep.tile([P, 1], F32)
        identity = keep.tile([P, P], F32)
        identity_bf16 = keep.tile([P, P], BF16)
        x_turned = keep.tile([P, len(TURNED), CI], BF16)
        result = keep.tile([P, GROUPS, L], F32)


        def load_turned(g):
            nc.sync.dma_start(out=w_raw[:, g], in_=w_quarters[g])

        def load_regrouped(g, first, count):
            channels = slice(first, first + count)
            nc.sync.dma_start(
                out=w_raw[:, g].rearrange("p (o n) -> p o n", o=CO)[:, channels, :],
                in_=w_fours[g, :, channels, :],
            )

        t0, t1 = TURNED
        r0, r1 = REGROUPED
        for road in (TURNED, REGROUPED):
            groups = slice(road[0], road[-1] + 1)
            nc.sync.dma_start(
                out=x_raw[:, groups].rearrange("p g j l -> p g (j l)"), in_=x_fours[:, groups]
            )
        load_turned(t0)
        nc.sync.dma_start(out=bias_rows[:].rearrange("g o s -> g (o s)"), in_=bias_view)
        load_regrouped(r0, 0, 16)
        load_turned(t1)
        load_regrouped(r0, 16, 8)
        load_regrouped(r0, 24, 8)
        load_regrouped(r1, 0, 16)
        load_regrouped(r1, 16, 12)
        load_regrouped(r1, 28, 4)

        def turn(g, word_list):
            words = w_raw[:, g].bitcast(F32).rearrange("p (c w) -> p c w", w=PAIRS)
            bank = turned.tile([P, BANK_WORDS * P], F32, name="bank")
            for slot, w in enumerate(word_list):
                nc.tensor.transpose(
                    bank[:, slot * P : (slot + 1) * P], words[:, :, w], identity[:]
                )
            return bank[:].bitcast(BF16)

        def turn_straddling(g, copy):
            halves = turn(g, STRADDLING).rearrange("p (w n e) -> p w e n", w=BANK_WORDS, e=2)
            copy(out=w_grouped[:, g, TAPS - 1, 0:SEGMENTS:2, :], in_=halves[:, 0:2, 0, :])
            copy(out=w_grouped[:, g, 0, 1:SEGMENTS:2, :], in_=halves[:, 0:2, 1, :])

        def turn_parity(g, bank_number, copy):
            parity, f0 = PARITY_BANKS[bank_number]
            word_list = [
                (TAPS * s + f) // 2 for f in (f0, f0 + 2) for s in range(parity, SEGMENTS, 2)
            ]
            halves = turn(g, word_list).rearrange("p (k a n e) -> p k a e n", k=2, a=2, e=2)
            target = w_grouped[:, g, f0 : f0 + 4, parity:SEGMENTS:2, :].rearrange(
                "p (k e) a n -> p k a e n", e=2
            )
            copy(out=target, in_=halves)

        def regroup_weights(copy, g, first, count, runs=REGROUP_RUNS):
            target = w_grouped[:, g]
            rows = slice(first * PACK, (first + count) * PACK)
            out_rows = rows
            if g == REGROUPED[-1]:
                half, inside = divmod(first, HALF)
                target = h_grouped[:, half]
                out_rows = slice(inside * PACK, (inside + count) * PACK)
            loaded = w_raw[:, g].rearrange("p (r s f) -> p r s f", s=SEGMENTS, f=TAPS)
            for f0, n in runs:
                taps = slice(f0, f0 + n)
                copy(
                    out=target[:, taps, :, out_rows].rearrange("p f s r -> p s r f"),
                    in_=loaded[:, rows, :, taps].rearrange("p r s f -> p s r f"),
                )

        def quantise_weights(g, runs):
            for f0, n in runs:
                taps = slice(f0, f0 + n)
                nc.vector.quantize_mx(
                    out=w_codes[:, g, taps].rearrange("p f n -> p (f n)").bitcast(FP8X4),
                    scales=w_scales[:, g, taps].rearrange("p f n -> p (f n)"),
                    in_=w_grouped[:, g, taps].rearrange("p f s n -> p (f s n)"),
                )

        def quantise_half(half, runs):
            first = half * (TAPS + 1)
            for f0, n in runs:
                taps = slice(first + f0, first + f0 + n)
                nc.vector.quantize_mx(
                    out=h_codes[:, taps].rearrange("p f n -> p (f n)").bitcast(FP8X4),
                    scales=h_scales[:, taps].rearrange("p f n -> p (f n)"),
                    in_=h_grouped[:, half, f0 : f0 + n].rearrange("p f s n -> p (f s n)"),
                )

        def convolve_half(half):
            acc = sums.tile([P, L], F32, name="acc")
            g = REGROUPED[-1]
            codes = h_codes[:].rearrange("p f n -> p (f n)")
            scales = h_scales[:].rearrange("p f n -> p (f n)")
            for f in range(TAPS):
                plane = f % PLANES
                start = (half * TAPS + f) * HALF_COLUMNS
                nc.tensor.matmul_mx(
                    out=acc[:],
                    lhsT=codes[:, start : start + P].bitcast(FP8X4),
                    lhsT_scale=scales[:, start : start + P],
                    rhs=x_codes[:, g, f * STEP : f * STEP + L].bitcast(FP8X4),
                    rhs_scale=x_scales[:, plane, g, (f - plane) * STEP : (f - plane) * STEP + L],
                    start=(f == 0),
                    stop=(f == TAPS - 1),
                )
            return acc

        def finish_half(half, acc):
            g = REGROUPED[-1]
            rows = slice(half * HALF_COLUMNS, (half + 1) * HALF_COLUMNS)
            nc.scalar.activation(
                out=result[rows, g, :].rearrange("p (q r) -> p q r", r=PHASES),
                in_=acc[rows].rearrange("p (r q) -> p q r", q=STEP),
                func=mybir.ActivationFunctionType.Identity,
                bias=bias_half_column[rows],
            )
            for s in range(SEGMENTS):
                positions = slice(SEG_START[s], SEG_START[s + 1])
                first = half * HALF_COLUMNS + s * HALF
                nc.sync.dma_start(
                    out=out_view[g, half * HALF : (half + 1) * HALF, positions],
                    in_=result[first : first + HALF, g, positions],
                )

        def convolve(g):
            acc = sums.tile([P, L], F32, name="acc")
            for f in range(TAPS):
                plane = f % PLANES
                nc.tensor.matmul_mx(
                    out=acc[:],
                    lhsT=w_codes[:, g, f, :].bitcast(FP8X4),
                    lhsT_scale=w_scales[:, g, f, :],
                    rhs=x_codes[:, g, f * STEP : f * STEP + L].bitcast(FP8X4),
                    rhs_scale=x_scales[:, plane, g, (f - plane) * STEP : (f - plane) * STEP + L],
                    start=(f == 0),
                    stop=(f == TAPS - 1),
                )
            return acc

        def fetch(g, acc):
            nc.scalar.activation(
                out=result[:, g, :].rearrange("p (q r) -> p q r", r=PHASES),
                in_=acc[:].rearrange("p (r q) -> p q r", q=STEP),
                func=mybir.ActivationFunctionType.Identity,
                bias=bias_column[:, g : g + 1],
            )

        def store(groups):
            for s in range(SEGMENTS):
                positions = slice(SEG_START[s], SEG_START[s + 1])
                nc.sync.dma_start(
                    out=out_view[groups, :, positions].rearrange("g o l -> o g l"),
                    in_=result[s * CO : (s + 1) * CO, groups, positions],
                )

        vector = nc.vector.tensor_copy
        scalar = nc.scalar.copy

        with tc.manual_schedule():
            make_identity(nc, identity[:])
            nc.vector.tensor_copy(out=identity_bf16[:], in_=identity[:])
            codes = x_codes[:].bitcast(I32).rearrange("p g (a q) -> p g a q", q=STEP)
            scales = x_scales[:, 0].rearrange("p g (a q) -> p g a q", q=STEP)
            nc.vector.memset(bias_sorted[:], 0.0)
            nc.vector.memset(bias_by_half[:], 0.0)
            nc.vector.memset(h_codes[:, TAPS].bitcast(I32), 0)
            nc.vector.memset(h_scales[:, TAPS].bitcast(I32), 0)
            nc.vector.memset(codes[:, :, 0:PAD], 0)
            nc.vector.memset(codes[:, :, PAD + PHASES :], 0)
            nc.vector.memset(x_scales[:, 0].rearrange("p g l -> p (g l)").bitcast(I32), 0)
            nc.scalar.activation(
                out=table_loaded[:],
                in_=identity[:, 0:1],
                func=mybir.ActivationFunctionType.Identity,
            )

            columns = x_grouped[:].rearrange("p g (r q) j -> p g r q j", q=STEP)

            def transpose_x(parts):
                bank = turned.tile([P, BANK_WORDS * P], F32, name="bank")
                halves = bank[:].bitcast(BF16)[:, 0 : PACK * P]
                for j, part in enumerate(parts):
                    nc.tensor.transpose(halves[:, j * P : (j + 1) * P], part, identity_bf16[:])
                return halves

            for g in TURNED:
                by_position = transpose_x([x_raw[:, g, j, :] for j in range(PACK)])
                nc.scalar.copy(
                    out=x_turned[:, g].rearrange("l (p j) -> l p j", j=PACK),
                    in_=by_position.rearrange("l (j p) -> l p j", j=PACK),
                )

            for g in TURNED:
                by_channel = transpose_x(
                    [x_turned[:, g, j * P : (j + 1) * P] for j in range(PACK)]
                )
                nc.scalar.copy(
                    out=columns[:, g], in_=by_channel.rearrange("p (j q r) -> p r q j", j=PACK, r=PHASES)
                )

            positions = x_raw[:].rearrange("p g j (q r) -> p g j q r", r=PHASES)
            groups = slice(REGROUPED[0], REGROUPED[-1] + 1)
            for first in range(0, PHASES, READ_RUN):
                run = slice(first, first + READ_RUN)
                nc.vector.tensor_copy(
                    out=columns[:, groups, run].rearrange("p g r q j -> p g q j r"),
                    in_=positions[:, groups, :, :, run].rearrange("p g j q r -> p g q j r"),
                )
            middle = slice(PAD * STEP, (PAD + PHASES) * STEP)
            for g in REGROUPED + TURNED:
                nc.vector.quantize_mx(
                    out=x_codes[:, g, middle].bitcast(FP8X4),
                    scales=x_scales[:, 0, g, middle],
                    in_=x_grouped[:, g].rearrange("p l j -> p (l j)"),
                )
            for rows in (codes, scales):
                nc.vector.tensor_copy(
                    out=rows[:, :, 0:PAD, 1:STEP], in_=rows[:, :, PHASES : PHASES + PAD, 0 : STEP - 1]
                )
                nc.vector.tensor_copy(
                    out=rows[:, :, PAD + PHASES :, 0 : STEP - 1], in_=rows[:, :, PAD : 2 * PAD, 1:STEP]
                )
            for plane in range(1, PLANES):
                nc.vector.tensor_copy(
                    out=x_scales[:, plane, :, 0 : TABLE - plane * STEP].bitcast(I32),
                    in_=x_scales[:, 0, :, plane * STEP : TABLE].bitcast(I32),
                )

            turn_straddling(t0, scalar)
            nc.scalar.copy(
                out=bias_sorted[0:GROUPS], in_=bias_rows[:].rearrange("g o s -> g s o")
            )
            nc.scalar.copy(
                out=bias_by_half[0:GROUPS],
                in_=bias_rows[:].rearrange("g (h o) s -> g h s o", h=HALVES),
            )
            turn_parity(t0, 0, scalar)
            turn_parity(t0, 1, scalar)
            regroup_weights(vector, r0, 0, 16)
            quantise_weights(t0, SHORT_RUNS[0:1])
            turn_parity(t0, 2, scalar)
            turn_parity(t0, 3, vector)
            bias_t = sums.tile([P, L], F32, name="acc")
            nc.tensor.transpose(
                bias_t[:], bias_sorted[:].rearrange("p s o -> p (s o)"), identity[:]
            )
            bias_half_t = sums.tile([P, L], F32, name="acc")
            nc.tensor.transpose(
                bias_half_t[:], bias_by_half[:].rearrange("p h s o -> p (h s o)"), identity[:]
            )
            quantise_weights(t0, SHORT_RUNS[1:])
            nc.vector.tensor_copy(out=bias_column[:], in_=bias_t[:, 0:GROUPS])
            nc.vector.tensor_copy(
                out=bias_half_column[:], in_=bias_half_t[:, REGROUPED[-1] : REGROUPED[-1] + 1]
            )
            turn_straddling(t1, scalar)
            regroup_weights(vector, r0, 16, 8)
            turn_parity(t1, 0, scalar)
            turn_parity(t1, 1, scalar)
            regroup_weights(vector, r0, 24, 8)
            turn_parity(t1, 2, scalar)
            turn_parity(t1, 3, scalar)
            acc_t0 = convolve(t0)
            fetch(t0, acc_t0)
            quantise_weights(r0, LONG_RUNS)
            acc_r0 = convolve(r0)
            regroup_weights(vector, r1, 0, 16, REGROUP_RUNS[0:2])
            regroup_weights(scalar, r1, 0, 16, REGROUP_RUNS[2:3])
            fetch(r0, acc_r0)
            store(slice(t0, r0 + 1, r0 - t0))
            quantise_weights(t1, SHORT_RUNS)
            quantise_half(0, LONG_RUNS)
            acc_t1 = convolve(t1)
            acc_0 = convolve_half(0)
            regroup_weights(vector, r1, 16, 12, REGROUP_RUNS[0:1])
            regroup_weights(scalar, r1, 16, 12, REGROUP_RUNS[1:3])
            regroup_weights(vector, r1, 28, 4, REGROUP_RUNS[0:2])
            regroup_weights(scalar, r1, 28, 4, REGROUP_RUNS[2:3])
            fetch(t1, acc_t1)
            store(slice(t1, t1 + 1))
            finish_half(0, acc_0)
            quantise_half(1, SHORT_RUNS)
            acc_1 = convolve_half(1)
            finish_half(1, acc_1)
